import numpy as np
import ml_dtypes


def mxq(x, axis, fmt="e4m3"):
    dtype, down = {"e4m3": (ml_dtypes.float8_e4m3fn, 7), "e5m2": (ml_dtypes.float8_e5m2, 14)}[fmt]
    v = np.moveaxis(np.asarray(x, np.float32).astype(ml_dtypes.bfloat16).astype(np.float64), axis, -1)
    blocks = v.reshape(v.shape[:-1] + (-1, 32))
    amax = np.abs(blocks).max(-1, keepdims=True)
    byte = np.maximum(np.where(amax > 0, np.frexp(amax)[1] - 1 + 127, 0) - down, 1)
    scale = np.exp2(byte - 127.0)
    codes = (blocks / scale).astype(np.float32).astype(dtype).astype(np.float64)
    return np.moveaxis((codes * scale).reshape(v.shape), -1, axis)


WIDE = False


def mx_kscale(k):
    if not WIDE:
        return np.ones(k)
    levels = np.array([10, -10, 5, -5, 0])
    a = np.random.permutation(np.resize(levels, k // 512 * 4)).reshape(k // 512, 4)
    idx = np.arange(k)
    return np.exp2(a[idx // 512, idx % 128 // 32])


BF16 = ml_dtypes.bfloat16


def bf(x):
    return np.asarray(x, np.float32).astype(BF16)


def f64(x):
    return np.asarray(x).astype(np.float64)


E2M1 = np.array([0.0, 0.5, 1.0, 1.5, 2.0, 3.0, 4.0, 6.0, -0.0, -0.5, -1.0, -1.5, -2.0, -3.0, -4.0, -6.0])


def pack_weight(w, fmt):
    k, n = w.shape
    w = f64(bf(w)).reshape(k // 32, 32, n)
    amax = np.abs(w).max(1)
    if fmt == "e4m3":
        byte = np.frexp(amax)[1] - 1 + 127 - 7
    else:
        mant, ex = np.frexp(amax / 6.0)
        byte = np.where(mant > 0.5, ex, ex - 1) + 127
    byte = np.clip(np.where(amax > 0, byte, 1), 1, 254)
    scaled = (w * np.exp2(127.0 - byte)[:, None, :]).reshape(k, n).astype(np.float32)
    by_word = np.ascontiguousarray(scaled.reshape(k // 512, 128, 4, n).transpose(0, 1, 3, 2))
    if fmt == "e4m3":
        words = by_word.astype(ml_dtypes.float8_e4m3fn).view(np.uint8)
    else:
        c = by_word.astype(ml_dtypes.float4_e2m1fn).view(np.uint8) & 0xF
        words = c[..., 0::2] | (c[..., 1::2] << 4)
    return np.ascontiguousarray(words), np.ascontiguousarray(byte.astype(np.uint8).reshape(k // 512, 16, n))


def unpack_weight(words, scales, fmt):
    g, p, n, _ = words.shape
    if fmt == "e4m3":
        vals = np.ascontiguousarray(words).view(ml_dtypes.float8_e4m3fn).astype(np.float64)
    else:
        nib = np.empty((g, p, n, 4), np.uint8)
        nib[..., 0::2] = words & 0xF
        nib[..., 1::2] = words >> 4
        vals = E2M1[nib]
    vals = vals * np.repeat(np.exp2(scales.astype(np.float64) - 127.0), 8, axis=1)[..., None]
    return vals.transpose(0, 1, 3, 2).reshape(g * 512, n)


B, T, HP, WP, NH, D, DFF = 16, 8, 3, 4, 16, 1024, 4096
HW = HP * WP
D3 = D + D + D
EPS = 1e-6


def layer_norm(x, g, b):
    m = x.mean(-1, keepdims=True)
    v = np.square(x - m).mean(-1, keepdims=True)
    return (x - m) / np.sqrt(v + EPS) * g + b


def setup_inputs():
    s = mx_kscale(D)
    x_res = bf(np.random.standard_normal((B, 1 + HW * T, D)) * 1.1)
    ln1_g = bf((1.0 + 0.1 * np.random.standard_normal(D)) * s)
    ln1_b = bf(0.1 * np.random.standard_normal(D) * s)
    words, scales = pack_weight(np.random.standard_normal((D, D3)) / np.sqrt(D) / s[:, None], "e4m3")
    s_qkv_b = bf(0.1 * np.random.standard_normal(D3))
    return {"x_res": x_res,
            "ln1_g": ln1_g,
            "ln1_b": ln1_b,
            "s_qkv_w_words": words,
            "s_qkv_w_scales": scales,
            "s_qkv_b": s_qkv_b}


def reference(x_res, ln1_g, ln1_b, s_qkv_w_words, s_qkv_w_scales, s_qkv_b):
    x = f64(x_res)
    cls_rep = np.broadcast_to(x[:, 0:1, :], (B, T, D)).reshape(B * T, 1, D)
    xs = x[:, 1:, :].reshape(B, HW, T, D).swapaxes(1, 2).reshape(B * T, HW, D)
    xs = np.concatenate([cls_rep, xs], axis=1)
    y = layer_norm(xs, f64(ln1_g), f64(ln1_b))
    return (mxq(y, 2, "e4m3") @ unpack_weight(s_qkv_w_words, s_qkv_w_scales, "e4m3")) + f64(s_qkv_b)

@@ -1,0 +1,222 @@
+from contextlib import ExitStack
+
+import concourse.mybir as mybir
+from concourse.masks import make_identity
+
+F32 = mybir.dt.float32
+BF16 = mybir.dt.bfloat16
+U8 = mybir.dt.uint8
+U32 = mybir.dt.uint32
+I32 = mybir.dt.int32
+FP8X4 = mybir.dt.float8_e4m3fn_x4
+ALU = mybir.AluOpType
+ACT = mybir.ActivationFunctionType
+
+P = 128
+SAMPLES, FRAMES, PATCHES = 16, 8, 12
+SEQ = 1 + PATCHES
+D = 1024
+D3 = 3072
+PACK = 4
+K_PASS = P * PACK
+PASSES = D // K_PASS
+BANK = 512
+STORE_BANKS = 3
+EPS = 1e-6
+VECTOR_STATS_BUNCHES = 2
+
+FLOPS = 2 * P * SEQ * D * D3
+
+
+def tile_timesformerlayer_pb_kernel(
+    tc, x_res, ln1_g, ln1_b, s_qkv_w_words, s_qkv_w_scales, s_qkv_b, out
+):
+    nc = tc.nc
+    bunches = [[0]] + [[s, s + 1] for s in range(1, SEQ, 2)]
+
+    with ExitStack() as ctx:
+        const = ctx.enter_context(tc.tile_pool(name="const", bufs=1))
+        small = ctx.enter_context(tc.tile_pool(name="small", bufs=4))
+        work = ctx.enter_context(tc.tile_pool(name="work", bufs=2))
+        results = ctx.enter_context(tc.tile_pool(name="results", bufs=6))
+        psum_t = ctx.enter_context(tc.psum_pool(name="psum_t", bufs=4))
+        psum_a = ctx.enter_context(tc.psum_pool(name="psum_a", bufs=4))
+
+        eps_col = const.tile([P, 1], F32)
+        nc.vector.memset(eps_col[:], EPS)
+        warm = const.tile([P, 1], F32)
+        nc.scalar.activation(out=warm[:], in_=eps_col[:], func=ACT.Sqrt)
+
+        w_planes = const.tile([P, D3], U8, align_bytes=64)
+        nc.vector.memset(w_planes[:].bitcast(I32), 0)
+
+        ident = const.tile([P, P], F32)
+        make_identity(nc, ident[:])
+
+        x_sb = []
+        for s in range(SEQ):
+            x_tile = const.tile([P, D], BF16, name="x%d" % s)
+            x_sb.append(x_tile)
+
+        def load_x(s):
+            if s == 0:
+                rows = x_res[:, 0:1, :].to_broadcast([SAMPLES, FRAMES, D])
+            else:
+                first = 1 + (s - 1) * FRAMES
+                rows = x_res[:, first : first + FRAMES, :]
+            nc.sync.dma_start(out=x_sb[s][:], in_=rows)
+
+        load_x(0)
+        gain_bf = const.tile([P, PASSES, PACK], BF16)
+        shift_bf = const.tile([P, PASSES, PACK], BF16)
+        nc.sync.dma_start(out=gain_bf[:], in_=ln1_g.rearrange("(g p t) -> p g t", g=PASSES, p=P))
+        nc.sync.dma_start(out=shift_bf[:], in_=ln1_b.rearrange("(g p t) -> p g t", g=PASSES, p=P))
+        gain_col = const.tile([P, PASSES * PACK], F32)
+        shift_col = const.tile([P, PASSES * PACK], F32)
+        nc.vector.tensor_copy(out=gain_col[:], in_=gain_bf[:].rearrange("p g t -> p (g t)"))
+        nc.vector.tensor_copy(out=shift_col[:], in_=shift_bf[:].rearrange("p g t -> p (g t)"))
+        load_x(1)
+        load_x(2)
+
+        for q in range(4):
+            nc.sync.dma_start(
+                out=w_planes[32 * q : 32 * q + 4 * PASSES, :].bitcast(I32),
+                in_=s_qkv_w_scales[:, 4 * q : 4 * q + 4, :].bitcast(I32),
+            )
+        w_codes = const.tile([P, PASSES, D3], U32, align_bytes=64)
+        bias_all = const.tile([P, D3], BF16)
+        w_chunk = 2 * BANK
+        for c in range(D3 // w_chunk):
+            cols = slice(c * w_chunk, (c + 1) * w_chunk)
+            for g in range(PASSES):
+                words = s_qkv_w_words[g].rearrange("p n t -> p (n t)").bitcast(I32)
+                nc.sync.dma_start(out=w_codes[:, g, cols].bitcast(I32), in_=words[:, cols])
+            if c == 0:
+                nc.sync.dma_start(out=bias_all[:], in_=s_qkv_b.partition_broadcast(P))
+        for s in range(3, SEQ):
+            load_x(s)
+
+        negmean, rstd, xhat, y_codes, y_planes = {}, {}, {}, {}, {}
+
+        def statistics(b):
+            tiles = bunches[b]
+            n = len(tiles)
+            negmean[b] = small.tile([P, n], F32, tag="negmean", name="negmean%d" % b)
+            rstd[b] = small.tile([P, n], F32, tag="rstd", name="rstd%d" % b)
+            std = small.tile([P, n], F32, tag="std")
+            if b < VECTOR_STATS_BUNCHES:
+                for i, s in enumerate(tiles):
+                    parts = small.tile([P, PASSES, 6], F32, tag="parts")
+                    for h in range(PASSES):
+                        nc.vector.bn_stats(out=parts[:, h, :], in_=x_sb[s][:, h * K_PASS : (h + 1) * K_PASS])
+                    mean_var = small.tile([P, 2], F32, tag="mean_var")
+                    nc.vector.bn_aggr(out=mean_var[:], in_=parts[:].rearrange("p h c -> p (h c)"))
+                    nc.vector.tensor_scalar_mul(out=negmean[b][:, i : i + 1], in0=mean_var[:, 0:1], scalar1=-1.0)
+                    nc.scalar.activation(
+                        out=std[:, i : i + 1], in_=mean_var[:, 1:2], func=ACT.Sqrt, bias=eps_col[:], scale=1.0
+                    )
+            else:
+                rowsum = small.tile([P, n], F32, tag="rowsum")
+                sumsq = small.tile([P, n], F32, tag="sumsq")
+                for i, s in enumerate(tiles):
+                    unread = work.tile([P, D], BF16, tag="unread", bufs=4)
+                    nc.scalar.activation(
+                        out=unread[:], in_=x_sb[s][:], func=ACT.Identity, accum_out=rowsum[:, i : i + 1]
+                    )
+                nc.scalar.mul(negmean[b][:], rowsum[:], -1.0 / D)
+                for i, s in enumerate(tiles):
+                    unread = work.tile([P, D], BF16, tag="unread", bufs=4)
+                    nc.scalar.activation(
+                        out=unread[:],
+                        in_=x_sb[s][:],
+                        func=ACT.Square,
+                        bias=negmean[b][:, i : i + 1],
+                        accum_out=sumsq[:, i : i + 1],
+                    )
+                nc.scalar.activation(out=std[:], in_=sumsq[:], func=ACT.Sqrt, bias=eps_col[:], scale=1.0 / D)
+            nc.vector.reciprocal(out=rstd[b][:], in_=std[:])
+
+        def normalise(b):
+            xhat[b] = []
+            for i, s in enumerate(bunches[b]):
+                sorted_rows = work.tile([P, PASSES, PACK, P], F32, tag="xhat", bufs=4)
+                nc.gpsimd.tensor_scalar(
+                    out=sorted_rows[:],
+                    in0=x_sb[s][:].rearrange("r (g p t) -> r g t p", g=PASSES, t=PACK),
+                    scalar1=negmean[b][:, i : i + 1],
+                    scalar2=rstd[b][:, i : i + 1],
+                    op0=ALU.add,
+                    op1=ALU.mult,
+                )
+                xhat[b].append(sorted_rows)
+
+        def quantise(b):
+            n = len(bunches[b])
+            planar = work.tile([P, PASSES, PACK, n, P], BF16, tag="planar")
+            grouped = work.tile([P, PASSES, n * P, PACK], BF16, tag="grouped", align_bytes=64)
+            for g in range(PASSES):
+                for half in range(2):
+                    bank = psum_t.tile([P, 2, n, P], F32, tag="xt")
+                    for j in range(2):
+                        for i in range(n):
+                            nc.tensor.transpose(
+                                out=bank[:, j, i, :], in_=xhat[b][i][:, g, 2 * half + j, :], identity=ident[:]
+                            )
+                    for j in range(2):
+                        t = 2 * half + j
+                        c = g * PACK + t
+                        nc.scalar.activation(
+                            out=planar[:, g, t, :, :],
+                            in_=bank[:, j, :, :],
+                            func=ACT.Identity,
+                            scale=gain_col[:, c : c + 1],
+                            bias=shift_col[:, c : c + 1],
+                        )
+                nc.gpsimd.tensor_scalar(
+                    out=grouped[:, g, :, :],
+                    in0=planar[:, g, :, :, :].rearrange("p t i r -> p (i r) t"),
+                    scalar1=1.0,
+                    scalar2=0.0,
+                    op0=ALU.mult,
+                    op1=ALU.add,
+                )
+            y_codes[b] = const.tile([P, PASSES, n * P], U32, name="y_codes%d" % b, align_bytes=64)
+            y_planes[b] = const.tile([P, PASSES, n * P], U8, name="y_planes%d" % b, align_bytes=64)
+            nc.vector.quantize_mx(
+                out=y_codes[b][:].rearrange("p g c -> p (g c)").bitcast(FP8X4),
+                scales=y_planes[b][:].rearrange("p g c -> p (g c)"),
+                in_=grouped[:].rearrange("p g c t -> p (g c t)"),
+            )
+
+        def multiply(b):
+            for i, s in enumerate(bunches[b]):
+                rows = slice(i * P, (i + 1) * P)
+                for first in range(0, D3 // BANK, STORE_BANKS):
+                    result = results.tile([P, STORE_BANKS, BANK], F32, tag="result")
+                    for j in range(STORE_BANKS):
+                        cols = slice((first + j) * BANK, (first + j + 1) * BANK)
+                        acc = psum_a.tile([P, BANK], F32, tag="acc")
+                        for g in range(PASSES):
+                            nc.tensor.matmul_mx(
+                                out=acc[:],
+                                lhsT=y_codes[b][:, g, rows].bitcast(FP8X4),
+                                lhsT_scale=y_planes[b][:, g, rows],
+                                rhs=w_codes[:, g, cols].bitcast(FP8X4),
+                                rhs_scale=w_planes[4 * g : P, cols],
+                                start=(g == 0),
+                                stop=(g == PASSES - 1),
+                            )
+                        nc.vector.tensor_tensor(out=result[:, j, :], in0=acc[:], in1=bias_all[:, cols], op=ALU.add)
+                    nc.sync.dma_start(
+                        out=out[:, s, first * BANK : (first + STORE_BANKS) * BANK],
+                        in_=result[:].rearrange("p j c -> p (j c)"),
+                    )
+
+        for step in range(len(bunches) + 2):
+            if step < len(bunches):
+                statistics(step)
+                normalise(step)
+            if 1 <= step <= len(bunches):
+                quantise(step - 1)
+            if step >= 2:
+                multiply(step - 2)

@@ -21,9 +21,11 @@ PACK = 4
 K_PASS = P * PACK
 PASSES = D // K_PASS
 BANK = 512
+BANKS = D3 // BANK
 STORE_BANKS = 3
 EPS = 1e-6
-VECTOR_STATS_BUNCHES = 2
+VECTOR_STATS_BUNCHES = 3
+EARLY_X = 5
 
 FLOPS = 2 * P * SEQ * D * D3
 
@@ -33,6 +35,7 @@ def tile_timesformerlayer_pb_kernel(
 ):
     nc = tc.nc
     bunches = [[0]] + [[s, s + 1] for s in range(1, SEQ, 2)]
+    n_bunches = len(bunches)
 
     with ExitStack() as ctx:
         const = ctx.enter_context(tc.tile_pool(name="const", bufs=1))
@@ -41,15 +44,24 @@ def tile_timesformerlayer_pb_kernel(
         results = ctx.enter_context(tc.tile_pool(name="results", bufs=6))
         psum_t = ctx.enter_context(tc.psum_pool(name="psum_t", bufs=4))
         psum_a = ctx.enter_context(tc.psum_pool(name="psum_a", bufs=4))
-
-        eps_col = const.tile([P, 1], F32)
-        nc.vector.memset(eps_col[:], EPS)
-        warm = const.tile([P, 1], F32)
-        nc.scalar.activation(out=warm[:], in_=eps_col[:], func=ACT.Sqrt)
+        ctx.enter_context(tc.manual_schedule())
 
         w_planes = const.tile([P, D3], U8, align_bytes=64)
         nc.vector.memset(w_planes[:].bitcast(I32), 0)
+        eps_col = const.tile([P, 1], F32)
+        nc.vector.memset(eps_col[:], EPS)
+        minus_half = const.tile([P, 2], F32)
+        nc.vector.memset(minus_half[:], -0.5)
+        ones = const.tile([P, P], BF16)
+        nc.vector.memset(ones[:], 1.0)
+        bias_row = const.tile([P, D3], BF16)
+        nc.vector.memset(bias_row[:], 0.0)
 
+        gain_bf = const.tile([P, PASSES, PACK], BF16)
+        shift_bf = const.tile([P, PASSES, PACK], BF16)
+        nc.gpsimd.dma_start(out=gain_bf[:], in_=ln1_g.rearrange("(g p t) -> p g t", g=PASSES, p=P))
+        nc.gpsimd.dma_start(out=shift_bf[:], in_=ln1_b.rearrange("(g p t) -> p g t", g=PASSES, p=P))
+        nc.gpsimd.dma_start(out=bias_row[0:1, :], in_=s_qkv_b.unsqueeze(0))
         ident = const.tile([P, P], F32)
         make_identity(nc, ident[:])
 
@@ -66,44 +78,43 @@ def tile_timesformerlayer_pb_kernel(
                 rows = x_res[:, first : first + FRAMES, :]
             nc.sync.dma_start(out=x_sb[s][:], in_=rows)
 
-        load_x(0)
-        gain_bf = const.tile([P, PASSES, PACK], BF16)
-        shift_bf = const.tile([P, PASSES, PACK], BF16)
-        nc.sync.dma_start(out=gain_bf[:], in_=ln1_g.rearrange("(g p t) -> p g t", g=PASSES, p=P))
-        nc.sync.dma_start(out=shift_bf[:], in_=ln1_b.rearrange("(g p t) -> p g t", g=PASSES, p=P))
-        gain_col = const.tile([P, PASSES * PACK], F32)
-        shift_col = const.tile([P, PASSES * PACK], F32)
-        nc.vector.tensor_copy(out=gain_col[:], in_=gain_bf[:].rearrange("p g t -> p (g t)"))
-        nc.vector.tensor_copy(out=shift_col[:], in_=shift_bf[:].rearrange("p g t -> p (g t)"))
-        load_x(1)
-        load_x(2)
-
+        for s in range(EARLY_X):
+            load_x(s)
         for q in range(4):
             nc.sync.dma_start(
                 out=w_planes[32 * q : 32 * q + 4 * PASSES, :].bitcast(I32),
                 in_=s_qkv_w_scales[:, 4 * q : 4 * q + 4, :].bitcast(I32),
             )
         w_codes = const.tile([P, PASSES, D3], U32, align_bytes=64)
-        bias_all = const.tile([P, D3], BF16)
         w_chunk = 2 * BANK
         for c in range(D3 // w_chunk):
             cols = slice(c * w_chunk, (c + 1) * w_chunk)
             for g in range(PASSES):
                 words = s_qkv_w_words[g].rearrange("p n t -> p (n t)").bitcast(I32)
                 nc.sync.dma_start(out=w_codes[:, g, cols].bitcast(I32), in_=words[:, cols])
-            if c == 0:
-                nc.sync.dma_start(out=bias_all[:], in_=s_qkv_b.partition_broadcast(P))
-        for s in range(3, SEQ):
+        for s in range(EARLY_X, SEQ):
             load_x(s)
 
-        negmean, rstd, xhat, y_codes, y_planes = {}, {}, {}, {}, {}
+        gain_col = const.tile([P, PASSES * PACK], F32)
+        shift_col = const.tile([P, PASSES * PACK], F32)
+        nc.vector.tensor_copy(out=gain_col[:], in_=gain_bf[:].rearrange("p g t -> p (g t)"))
+        nc.vector.tensor_copy(out=shift_col[:], in_=shift_bf[:].rearrange("p g t -> p (g t)"))
+        bias_all = const.tile([P, D3], F32)
+
+        def spread_bias():
+            for j in range(BANKS):
+                cols = slice(j * BANK, (j + 1) * BANK)
+                acc = psum_a.tile([P, BANK], F32, tag="acc")
+                nc.tensor.matmul(out=acc[:], lhsT=ones[:], rhs=bias_row[:, cols], start=True, stop=True)
+                nc.scalar.copy(out=bias_all[:, cols], in_=acc[:])
+
+        negmean, var_eps, rstd, xhat, planar, y_codes, y_planes = {}, {}, {}, {}, {}, {}, {}
 
         def statistics(b):
             tiles = bunches[b]
             n = len(tiles)
             negmean[b] = small.tile([P, n], F32, tag="negmean", name="negmean%d" % b)
-            rstd[b] = small.tile([P, n], F32, tag="rstd", name="rstd%d" % b)
-            std = small.tile([P, n], F32, tag="std")
+            var_eps[b] = small.tile([P, n], F32, tag="var_eps", name="var_eps%d" % b)
             if b < VECTOR_STATS_BUNCHES:
                 for i, s in enumerate(tiles):
                     parts = small.tile([P, PASSES, 6], F32, tag="parts")
@@ -112,9 +123,7 @@ def tile_timesformerlayer_pb_kernel(
                     mean_var = small.tile([P, 2], F32, tag="mean_var")
                     nc.vector.bn_aggr(out=mean_var[:], in_=parts[:].rearrange("p h c -> p (h c)"))
                     nc.vector.tensor_scalar_mul(out=negmean[b][:, i : i + 1], in0=mean_var[:, 0:1], scalar1=-1.0)
-                    nc.scalar.activation(
-                        out=std[:, i : i + 1], in_=mean_var[:, 1:2], func=ACT.Sqrt, bias=eps_col[:], scale=1.0
-                    )
+                    nc.vector.tensor_scalar_add(out=var_eps[b][:, i : i + 1], in0=mean_var[:, 1:2], scalar1=EPS)
             else:
                 rowsum = small.tile([P, n], F32, tag="rowsum")
                 sumsq = small.tile([P, n], F32, tag="sumsq")
@@ -133,10 +142,14 @@ def tile_timesformerlayer_pb_kernel(
                         bias=negmean[b][:, i : i + 1],
                         accum_out=sumsq[:, i : i + 1],
                     )
-                nc.scalar.activation(out=std[:], in_=sumsq[:], func=ACT.Sqrt, bias=eps_col[:], scale=1.0 / D)
-            nc.vector.reciprocal(out=rstd[b][:], in_=std[:])
+                nc.scalar.activation(
+                    out=var_eps[b][:], in_=sumsq[:], func=ACT.Identity, bias=eps_col[:], scale=1.0 / D
+                )
 
         def normalise(b):
+            n = len(bunches[b])
+            rstd[b] = small.tile([P, n], F32, tag="rstd", name="rstd%d" % b)
+            nc.gpsimd.tensor_tensor(out=rstd[b][:], in0=var_eps[b][:], in1=minus_half[:, 0:n], op=ALU.pow)
             xhat[b] = []
             for i, s in enumerate(bunches[b]):
                 sorted_rows = work.tile([P, PASSES, PACK, P], F32, tag="xhat", bufs=4)
@@ -150,10 +163,9 @@ def tile_timesformerlayer_pb_kernel(
                 )
                 xhat[b].append(sorted_rows)
 
-        def quantise(b):
+        def transpose(b):
             n = len(bunches[b])
-            planar = work.tile([P, PASSES, PACK, n, P], BF16, tag="planar")
-            grouped = work.tile([P, PASSES, n * P, PACK], BF16, tag="grouped", align_bytes=64)
+            planar[b] = work.tile([P, PASSES, PACK, n, P], BF16, tag="planar", name="planar%d" % b)
             for g in range(PASSES):
                 for half in range(2):
                     bank = psum_t.tile([P, 2, n, P], F32, tag="xt")
@@ -166,57 +178,82 @@ def tile_timesformerlayer_pb_kernel(
                         t = 2 * half + j
                         c = g * PACK + t
                         nc.scalar.activation(
-                            out=planar[:, g, t, :, :],
+                            out=planar[b][:, g, t, :, :],
                             in_=bank[:, j, :, :],
                             func=ACT.Identity,
                             scale=gain_col[:, c : c + 1],
                             bias=shift_col[:, c : c + 1],
                         )
+
+        grouped = {}
+
+        def regroup(b):
+            n = len(bunches[b])
+            grouped[b] = work.tile(
+                [P, PASSES, n * P, PACK], BF16, tag="grouped", name="grouped%d" % b, align_bytes=64
+            )
+            for g in range(PASSES):
                 nc.gpsimd.tensor_scalar(
-                    out=grouped[:, g, :, :],
-                    in0=planar[:, g, :, :, :].rearrange("p t i r -> p (i r) t"),
+                    out=grouped[b][:, g, :, :],
+                    in0=planar[b][:, g, :, :, :].rearrange("p t i r -> p (i r) t"),
                     scalar1=1.0,
                     scalar2=0.0,
                     op0=ALU.mult,
                     op1=ALU.add,
                 )
+
+        def quantise(b):
+            n = len(bunches[b])
             y_codes[b] = const.tile([P, PASSES, n * P], U32, name="y_codes%d" % b, align_bytes=64)
             y_planes[b] = const.tile([P, PASSES, n * P], U8, name="y_planes%d" % b, align_bytes=64)
             nc.vector.quantize_mx(
                 out=y_codes[b][:].rearrange("p g c -> p (g c)").bitcast(FP8X4),
                 scales=y_planes[b][:].rearrange("p g c -> p (g c)"),
-                in_=grouped[:].rearrange("p g c t -> p (g c t)"),
+                in_=grouped[b][:].rearrange("p g c t -> p (g c t)"),
             )
 
-        def multiply(b):
-            for i, s in enumerate(bunches[b]):
-                rows = slice(i * P, (i + 1) * P)
-                for first in range(0, D3 // BANK, STORE_BANKS):
-                    result = results.tile([P, STORE_BANKS, BANK], F32, tag="result")
-                    for j in range(STORE_BANKS):
-                        cols = slice((first + j) * BANK, (first + j + 1) * BANK)
-                        acc = psum_a.tile([P, BANK], F32, tag="acc")
-                        for g in range(PASSES):
-                            nc.tensor.matmul_mx(
-                                out=acc[:],
-                                lhsT=y_codes[b][:, g, rows].bitcast(FP8X4),
-                                lhsT_scale=y_planes[b][:, g, rows],
-                                rhs=w_codes[:, g, cols].bitcast(FP8X4),
-                                rhs_scale=w_planes[4 * g : P, cols],
-                                start=(g == 0),
-                                stop=(g == PASSES - 1),
-                            )
-                        nc.vector.tensor_tensor(out=result[:, j, :], in0=acc[:], in1=bias_all[:, cols], op=ALU.add)
-                    nc.sync.dma_start(
-                        out=out[:, s, first * BANK : (first + STORE_BANKS) * BANK],
-                        in_=result[:].rearrange("p j c -> p (j c)"),
+        def multiply(b, i, first):
+            s = bunches[b][i]
+            rows = slice(i * P, (i + 1) * P)
+            result = results.tile([P, STORE_BANKS, BANK], F32, tag="result")
+            for j in range(STORE_BANKS):
+                cols = slice((first + j) * BANK, (first + j + 1) * BANK)
+                acc = psum_a.tile([P, BANK], F32, tag="acc")
+                for g in range(PASSES):
+                    nc.tensor.matmul_mx(
+                        out=acc[:],
+                        lhsT=y_codes[b][:, g, rows].bitcast(FP8X4),
+                        lhsT_scale=y_planes[b][:, g, rows],
+                        rhs=w_codes[:, g, cols].bitcast(FP8X4),
+                        rhs_scale=w_planes[4 * g : P, cols],
+                        start=(g == 0),
+                        stop=(g == PASSES - 1),
                     )
+                nc.vector.tensor_tensor(out=result[:, j, :], in0=acc[:], in1=bias_all[:, cols], op=ALU.add)
+            nc.sync.dma_start(
+                out=out[:, s, first * BANK : (first + STORE_BANKS) * BANK],
+                in_=result[:].rearrange("p j c -> p (j c)"),
+            )
 
-        for step in range(len(bunches) + 2):
-            if step < len(bunches):
-                statistics(step)
-                normalise(step)
-            if 1 <= step <= len(bunches):
-                quantise(step - 1)
-            if step >= 2:
-                multiply(step - 2)
+        for b in range(VECTOR_STATS_BUNCHES):
+            statistics(b)
+        for b in range(-2, n_bunches):
+            if 0 <= b + 1 < n_bunches:
+                transpose(b + 1)
+            if b == -1:
+                spread_bias()
+            if b + 2 < n_bunches:
+                normalise(b + 2)
+            if 0 <= b + 1 < n_bunches:
+                regroup(b + 1)
+            pieces = []
+            if b >= 0:
+                pieces = [(i, first) for i in range(len(bunches[b])) for first in range(0, BANKS, STORE_BANKS)]
+            for i, first in pieces[:-1]:
+                multiply(b, i, first)
+            if 0 <= b + 1 < n_bunches:
+                quantise(b + 1)
+            for i, first in pieces[-1:]:
+                multiply(b, i, first)
+            if VECTOR_STATS_BUNCHES <= b + 3 < n_bunches:
+                statistics(b + 3)

@@ -24,7 +24,13 @@ BANK = 512
 BANKS = D3 // BANK
 STORE_BANKS = 3
 EPS = 1e-6
-VECTOR_STATS_BUNCHES = 3
+
+AHEAD_STATISTICS = 5
+AHEAD_NORMALISE = 3
+AHEAD_TRANSPOSE = 2
+AHEAD_QUANTISE = 1
+VECTOR_STATISTICS = 5
+VECTOR_REGROUPS = 2
 EARLY_X = 5
 
 FLOPS = 2 * P * SEQ * D * D3
@@ -34,36 +40,34 @@ def tile_timesformerlayer_pb_kernel(
     tc, x_res, ln1_g, ln1_b, s_qkv_w_words, s_qkv_w_scales, s_qkv_b, out
 ):
     nc = tc.nc
-    bunches = [[0]] + [[s, s + 1] for s in range(1, SEQ, 2)]
-    n_bunches = len(bunches)
 
     with ExitStack() as ctx:
         const = ctx.enter_context(tc.tile_pool(name="const", bufs=1))
-        small = ctx.enter_context(tc.tile_pool(name="small", bufs=4))
-        work = ctx.enter_context(tc.tile_pool(name="work", bufs=2))
+        small = ctx.enter_context(tc.tile_pool(name="small", bufs=6))
+        work = ctx.enter_context(tc.tile_pool(name="work", bufs=3))
         results = ctx.enter_context(tc.tile_pool(name="results", bufs=6))
-        psum_t = ctx.enter_context(tc.psum_pool(name="psum_t", bufs=4))
-        psum_a = ctx.enter_context(tc.psum_pool(name="psum_a", bufs=4))
+        psum_t = ctx.enter_context(tc.psum_pool(name="psum_t", bufs=3))
+        psum_a = ctx.enter_context(tc.psum_pool(name="psum_a", bufs=5))
         ctx.enter_context(tc.manual_schedule())
 
+        bias_row = const.tile([P, D3], BF16)
+        nc.vector.memset(bias_row[:].bitcast(I32), 0)
         w_planes = const.tile([P, D3], U8, align_bytes=64)
         nc.vector.memset(w_planes[:].bitcast(I32), 0)
-        eps_col = const.tile([P, 1], F32)
-        nc.vector.memset(eps_col[:], EPS)
-        minus_half = const.tile([P, 2], F32)
-        nc.vector.memset(minus_half[:], -0.5)
         ones = const.tile([P, P], BF16)
         nc.vector.memset(ones[:], 1.0)
-        bias_row = const.tile([P, D3], BF16)
-        nc.vector.memset(bias_row[:], 0.0)
+        eps_col = const.tile([P, 1], F32)
+        nc.vector.memset(eps_col[:], EPS)
+        minus_half = const.tile([P, 1], F32)
+        nc.vector.memset(minus_half[:], -0.5)
+        ident = const.tile([P, P], F32)
+        make_identity(nc, ident[:])
 
         gain_bf = const.tile([P, PASSES, PACK], BF16)
         shift_bf = const.tile([P, PASSES, PACK], BF16)
-        nc.gpsimd.dma_start(out=gain_bf[:], in_=ln1_g.rearrange("(g p t) -> p g t", g=PASSES, p=P))
-        nc.gpsimd.dma_start(out=shift_bf[:], in_=ln1_b.rearrange("(g p t) -> p g t", g=PASSES, p=P))
-        nc.gpsimd.dma_start(out=bias_row[0:1, :], in_=s_qkv_b.unsqueeze(0))
-        ident = const.tile([P, P], F32)
-        make_identity(nc, ident[:])
+        nc.scalar.dma_start(out=bias_row[0:1, :], in_=s_qkv_b.unsqueeze(0))
+        nc.scalar.dma_start(out=gain_bf[:], in_=ln1_g.rearrange("(g p t) -> p g t", g=PASSES, p=P))
+        nc.scalar.dma_start(out=shift_bf[:], in_=ln1_b.rearrange("(g p t) -> p g t", g=PASSES, p=P))
 
         x_sb = []
         for s in range(SEQ):
@@ -95,165 +99,122 @@ def tile_timesformerlayer_pb_kernel(
         for s in range(EARLY_X, SEQ):
             load_x(s)
 
+        bias_all = const.tile([P, D3], F32)
+        for j in range(BANKS):
+            cols = slice(j * BANK, (j + 1) * BANK)
+            acc = psum_a.tile([P, BANK], F32, tag="acc")
+            nc.tensor.matmul(out=acc[:], lhsT=ones[:], rhs=bias_row[:, cols], start=True, stop=True)
+            nc.scalar.copy(out=bias_all[:, cols], in_=acc[:])
         gain_col = const.tile([P, PASSES * PACK], F32)
         shift_col = const.tile([P, PASSES * PACK], F32)
-        nc.vector.tensor_copy(out=gain_col[:], in_=gain_bf[:].rearrange("p g t -> p (g t)"))
-        nc.vector.tensor_copy(out=shift_col[:], in_=shift_bf[:].rearrange("p g t -> p (g t)"))
-        bias_all = const.tile([P, D3], F32)
+        nc.scalar.copy(out=gain_col[:], in_=gain_bf[:].rearrange("p g t -> p (g t)"))
+        nc.scalar.copy(out=shift_col[:], in_=shift_bf[:].rearrange("p g t -> p (g t)"))
 
-        def spread_bias():
-            for j in range(BANKS):
-                cols = slice(j * BANK, (j + 1) * BANK)
-                acc = psum_a.tile([P, BANK], F32, tag="acc")
-                nc.tensor.matmul(out=acc[:], lhsT=ones[:], rhs=bias_row[:, cols], start=True, stop=True)
-                nc.scalar.copy(out=bias_all[:, cols], in_=acc[:])
+        negmean, var_eps, xhat, planar, grouped, y_codes, y_planes = {}, {}, {}, {}, {}, {}, {}
 
-        negmean, var_eps, rstd, xhat, planar, y_codes, y_planes = {}, {}, {}, {}, {}, {}, {}
-
-        def statistics(b):
-            tiles = bunches[b]
-            n = len(tiles)
-            negmean[b] = small.tile([P, n], F32, tag="negmean", name="negmean%d" % b)
-            var_eps[b] = small.tile([P, n], F32, tag="var_eps", name="var_eps%d" % b)
-            if b < VECTOR_STATS_BUNCHES:
-                for i, s in enumerate(tiles):
-                    parts = small.tile([P, PASSES, 6], F32, tag="parts")
-                    for h in range(PASSES):
-                        nc.vector.bn_stats(out=parts[:, h, :], in_=x_sb[s][:, h * K_PASS : (h + 1) * K_PASS])
-                    mean_var = small.tile([P, 2], F32, tag="mean_var")
-                    nc.vector.bn_aggr(out=mean_var[:], in_=parts[:].rearrange("p h c -> p (h c)"))
-                    nc.vector.tensor_scalar_mul(out=negmean[b][:, i : i + 1], in0=mean_var[:, 0:1], scalar1=-1.0)
-                    nc.vector.tensor_scalar_add(out=var_eps[b][:, i : i + 1], in0=mean_var[:, 1:2], scalar1=EPS)
+        def statistics(s):
+            negmean[s] = small.tile([P, 1], F32, tag="negmean", name="negmean%d" % s)
+            var_eps[s] = small.tile([P, 1], F32, tag="var_eps", name="var_eps%d" % s)
+            if s < VECTOR_STATISTICS:
+                parts = small.tile([P, PASSES, 6], F32, tag="parts")
+                for h in range(PASSES):
+                    nc.vector.bn_stats(out=parts[:, h, :], in_=x_sb[s][:, h * K_PASS : (h + 1) * K_PASS])
+                mean_var = small.tile([P, 2], F32, tag="mean_var")
+                nc.vector.bn_aggr(out=mean_var[:], in_=parts[:].rearrange("p h c -> p (h c)"))
+                nc.vector.tensor_scalar_mul(out=negmean[s][:], in0=mean_var[:, 0:1], scalar1=-1.0)
+                nc.vector.tensor_scalar_add(out=var_eps[s][:], in0=mean_var[:, 1:2], scalar1=EPS)
             else:
-                rowsum = small.tile([P, n], F32, tag="rowsum")
-                sumsq = small.tile([P, n], F32, tag="sumsq")
-                for i, s in enumerate(tiles):
-                    unread = work.tile([P, D], BF16, tag="unread", bufs=4)
-                    nc.scalar.activation(
-                        out=unread[:], in_=x_sb[s][:], func=ACT.Identity, accum_out=rowsum[:, i : i + 1]
-                    )
-                nc.scalar.mul(negmean[b][:], rowsum[:], -1.0 / D)
-                for i, s in enumerate(tiles):
-                    unread = work.tile([P, D], BF16, tag="unread", bufs=4)
-                    nc.scalar.activation(
-                        out=unread[:],
-                        in_=x_sb[s][:],
-                        func=ACT.Square,
-                        bias=negmean[b][:, i : i + 1],
-                        accum_out=sumsq[:, i : i + 1],
-                    )
+                rowsum = small.tile([P, 1], F32, tag="rowsum")
+                sumsq = small.tile([P, 1], F32, tag="sumsq")
+                unread = work.tile([P, D], BF16, tag="unread", bufs=4)
+                nc.scalar.activation(out=unread[:], in_=x_sb[s][:], func=ACT.Identity, accum_out=rowsum[:])
+                nc.scalar.mul(negmean[s][:], rowsum[:], -1.0 / D)
+                unread = work.tile([P, D], BF16, tag="unread", bufs=4)
                 nc.scalar.activation(
-                    out=var_eps[b][:], in_=sumsq[:], func=ACT.Identity, bias=eps_col[:], scale=1.0 / D
+                    out=unread[:], in_=x_sb[s][:], func=ACT.Square, bias=negmean[s][:], accum_out=sumsq[:]
+                )
+                nc.scalar.activation(
+                    out=var_eps[s][:], in_=sumsq[:], func=ACT.Identity, bias=eps_col[:], scale=1.0 / D
                 )
 
-        def normalise(b):
-            n = len(bunches[b])
-            rstd[b] = small.tile([P, n], F32, tag="rstd", name="rstd%d" % b)
-            nc.gpsimd.tensor_tensor(out=rstd[b][:], in0=var_eps[b][:], in1=minus_half[:, 0:n], op=ALU.pow)
-            xhat[b] = []
-            for i, s in enumerate(bunches[b]):
-                sorted_rows = work.tile([P, PASSES, PACK, P], F32, tag="xhat", bufs=4)
-                nc.gpsimd.tensor_scalar(
-                    out=sorted_rows[:],
-                    in0=x_sb[s][:].rearrange("r (g p t) -> r g t p", g=PASSES, t=PACK),
-                    scalar1=negmean[b][:, i : i + 1],
-                    scalar2=rstd[b][:, i : i + 1],
-                    op0=ALU.add,
-                    op1=ALU.mult,
-                )
-                xhat[b].append(sorted_rows)
-
-        def transpose(b):
-            n = len(bunches[b])
-            planar[b] = work.tile([P, PASSES, PACK, n, P], BF16, tag="planar", name="planar%d" % b)
-            for g in range(PASSES):
-                for half in range(2):
-                    bank = psum_t.tile([P, 2, n, P], F32, tag="xt")
-                    for j in range(2):
-                        for i in range(n):
-                            nc.tensor.transpose(
-                                out=bank[:, j, i, :], in_=xhat[b][i][:, g, 2 * half + j, :], identity=ident[:]
-                            )
-                    for j in range(2):
-                        t = 2 * half + j
-                        c = g * PACK + t
-                        nc.scalar.activation(
-                            out=planar[b][:, g, t, :, :],
-                            in_=bank[:, j, :, :],
-                            func=ACT.Identity,
-                            scale=gain_col[:, c : c + 1],
-                            bias=shift_col[:, c : c + 1],
-                        )
-
-        grouped = {}
-
-        def regroup(b):
-            n = len(bunches[b])
-            grouped[b] = work.tile(
-                [P, PASSES, n * P, PACK], BF16, tag="grouped", name="grouped%d" % b, align_bytes=64
-            )
-            for g in range(PASSES):
-                nc.gpsimd.tensor_scalar(
-                    out=grouped[b][:, g, :, :],
-                    in0=planar[b][:, g, :, :, :].rearrange("p t i r -> p (i r) t"),
-                    scalar1=1.0,
-                    scalar2=0.0,
-                    op0=ALU.mult,
-                    op1=ALU.add,
-                )
-
-        def quantise(b):
-            n = len(bunches[b])
-            y_codes[b] = const.tile([P, PASSES, n * P], U32, name="y_codes%d" % b, align_bytes=64)
-            y_planes[b] = const.tile([P, PASSES, n * P], U8, name="y_planes%d" % b, align_bytes=64)
-            nc.vector.quantize_mx(
-                out=y_codes[b][:].rearrange("p g c -> p (g c)").bitcast(FP8X4),
-                scales=y_planes[b][:].rearrange("p g c -> p (g c)"),
-                in_=grouped[b][:].rearrange("p g c t -> p (g c t)"),
+        def normalise(s):
+            rstd = small.tile([P, 1], F32, tag="rstd")
+            nc.gpsimd.tensor_tensor(out=rstd[:], in0=var_eps[s][:], in1=minus_half[:], op=ALU.pow)
+            xhat[s] = work.tile([P, PASSES, PACK, P], F32, tag="xhat", name="xhat%d" % s, bufs=4)
+            nc.gpsimd.tensor_scalar(
+                out=xhat[s][:],
+                in0=x_sb[s][:].rearrange("r (g p t) -> r g t p", g=PASSES, t=PACK),
+                scalar1=negmean[s][:],
+                scalar2=rstd[:],
+                op0=ALU.add,
+                op1=ALU.mult,
             )
 
-        def multiply(b, i, first):
-            s = bunches[b][i]
-            rows = slice(i * P, (i + 1) * P)
-            result = results.tile([P, STORE_BANKS, BANK], F32, tag="result")
-            for j in range(STORE_BANKS):
-                cols = slice((first + j) * BANK, (first + j + 1) * BANK)
-                acc = psum_a.tile([P, BANK], F32, tag="acc")
-                for g in range(PASSES):
-                    nc.tensor.matmul_mx(
-                        out=acc[:],
-                        lhsT=y_codes[b][:, g, rows].bitcast(FP8X4),
-                        lhsT_scale=y_planes[b][:, g, rows],
-                        rhs=w_codes[:, g, cols].bitcast(FP8X4),
-                        rhs_scale=w_planes[4 * g : P, cols],
-                        start=(g == 0),
-                        stop=(g == PASSES - 1),
+        def transpose(s):
+            planar[s] = work.tile([P, PASSES, PACK, P], BF16, tag="planar", name="planar%d" % s)
+            for g in range(PASSES):
+                bank = psum_t.tile([P, PACK, P], F32, tag="xt")
+                for t in range(PACK):
+                    nc.tensor.transpose(out=bank[:, t, :], in_=xhat[s][:, g, t, :], identity=ident[:])
+                for t in range(PACK):
+                    c = g * PACK + t
+                    nc.scalar.activation(
+                        out=planar[s][:, g, t, :],
+                        in_=bank[:, t, :],
+                        func=ACT.Identity,
+                        scale=gain_col[:, c : c + 1],
+                        bias=shift_col[:, c : c + 1],
                     )
-                nc.vector.tensor_tensor(out=result[:, j, :], in0=acc[:], in1=bias_all[:, cols], op=ALU.add)
-            nc.sync.dma_start(
-                out=out[:, s, first * BANK : (first + STORE_BANKS) * BANK],
-                in_=result[:].rearrange("p j c -> p (j c)"),
+
+        def quantise(s):
+            grouped[s] = work.tile([P, PASSES, P, PACK], BF16, tag="grouped", name="grouped%d" % s, align_bytes=64)
+            engine = nc.vector if s < VECTOR_REGROUPS else nc.gpsimd
+            engine.tensor_scalar(
+                out=grouped[s][:],
+                in0=planar[s][:].rearrange("p g t r -> p g r t"),
+                scalar1=1.0,
+                scalar2=0.0,
+                op0=ALU.mult,
+                op1=ALU.add,
+            )
+            y_codes[s] = const.tile([P, PASSES, P], U32, name="y_codes%d" % s, align_bytes=64)
+            y_planes[s] = const.tile([P, PASSES, P], U8, name="y_planes%d" % s, align_bytes=64)
+            nc.vector.quantize_mx(
+                out=y_codes[s][:].rearrange("p g r -> p (g r)").bitcast(FP8X4),
+                scales=y_planes[s][:].rearrange("p g r -> p (g r)"),
+                in_=grouped[s][:].rearrange("p g r t -> p (g r t)"),
             )
 
-        for b in range(VECTOR_STATS_BUNCHES):
-            statistics(b)
-        for b in range(-2, n_bunches):
-            if 0 <= b + 1 < n_bunches:
-                transpose(b + 1)
-            if b == -1:
-                spread_bias()
-            if b + 2 < n_bunches:
-                normalise(b + 2)
-            if 0 <= b + 1 < n_bunches:
-                regroup(b + 1)
-            pieces = []
-            if b >= 0:
-                pieces = [(i, first) for i in range(len(bunches[b])) for first in range(0, BANKS, STORE_BANKS)]
-            for i, first in pieces[:-1]:
-                multiply(b, i, first)
-            if 0 <= b + 1 < n_bunches:
-                quantise(b + 1)
-            for i, first in pieces[-1:]:
-                multiply(b, i, first)
-            if VECTOR_STATS_BUNCHES <= b + 3 < n_bunches:
-                statistics(b + 3)
+        def multiply(s):
+            for first in range(0, BANKS, STORE_BANKS):
+                result = results.tile([P, STORE_BANKS, BANK], F32, tag="result")
+                for j in range(STORE_BANKS):
+                    cols = slice((first + j) * BANK, (first + j + 1) * BANK)
+                    acc = psum_a.tile([P, BANK], F32, tag="acc")
+                    for g in range(PASSES):
+                        nc.tensor.matmul_mx(
+                            out=acc[:],
+                            lhsT=y_codes[s][:, g, :].bitcast(FP8X4),
+                            lhsT_scale=y_planes[s][:, g, :],
+                            rhs=w_codes[:, g, cols].bitcast(FP8X4),
+                            rhs_scale=w_planes[4 * g : P, cols],
+                            start=(g == 0),
+                            stop=(g == PASSES - 1),
+                        )
+                    nc.vector.tensor_tensor(out=result[:, j, :], in0=acc[:], in1=bias_all[:, cols], op=ALU.add)
+                nc.sync.dma_start(
+                    out=out[:, s, first * BANK : (first + STORE_BANKS) * BANK],
+                    in_=result[:].rearrange("p j c -> p (j c)"),
+                )
+
+        for s in range(-AHEAD_STATISTICS, SEQ):
+            if 0 <= s + AHEAD_TRANSPOSE < SEQ:
+                transpose(s + AHEAD_TRANSPOSE)
+            if 0 <= s + AHEAD_QUANTISE < SEQ:
+                quantise(s + AHEAD_QUANTISE)
+            if 0 <= s + AHEAD_NORMALISE < SEQ:
+                normalise(s + AHEAD_NORMALISE)
+            if s >= 0:
+                multiply(s)
+            if s + AHEAD_STATISTICS < SEQ:
+                statistics(s + AHEAD_STATISTICS)

@@ -121,8 +121,8 @@ def tile_timesformerlayer_pb_kernel(
                     nc.vector.bn_stats(out=parts[:, h, :], in_=x_sb[s][:, h * K_PASS : (h + 1) * K_PASS])
                 mean_var = small.tile([P, 2], F32, tag="mean_var")
                 nc.vector.bn_aggr(out=mean_var[:], in_=parts[:].rearrange("p h c -> p (h c)"))
-                nc.vector.tensor_scalar_mul(out=negmean[s][:], in0=mean_var[:, 0:1], scalar1=-1.0)
                 nc.vector.tensor_scalar_add(out=var_eps[s][:], in0=mean_var[:, 1:2], scalar1=EPS)
+                nc.vector.tensor_scalar_mul(out=negmean[s][:], in0=mean_var[:, 0:1], scalar1=-1.0)
             else:
                 rowsum = small.tile([P, 1], F32, tag="rowsum")
                 sumsq = small.tile([P, 1], F32, tag="sumsq")
@@ -186,9 +186,10 @@ def tile_timesformerlayer_pb_kernel(
             )
 
         def multiply(s):
-            for first in range(0, BANKS, STORE_BANKS):
-                result = results.tile([P, STORE_BANKS, BANK], F32, tag="result")
-                for j in range(STORE_BANKS):
+            store_banks = 1 if s == SEQ - 1 else STORE_BANKS
+            for first in range(0, BANKS, store_banks):
+                result = results.tile([P, store_banks, BANK], F32, tag="result")
+                for j in range(store_banks):
                     cols = slice((first + j) * BANK, (first + j + 1) * BANK)
                     acc = psum_a.tile([P, BANK], F32, tag="acc")
                     for g in range(PASSES):
@@ -203,7 +204,7 @@ def tile_timesformerlayer_pb_kernel(
                         )
                     nc.vector.tensor_tensor(out=result[:, j, :], in0=acc[:], in1=bias_all[:, cols], op=ALU.add)
                 nc.sync.dma_start(
-                    out=out[:, s, first * BANK : (first + STORE_BANKS) * BANK],
+                    out=out[:, s, first * BANK : (first + store_banks) * BANK],
                     in_=result[:].rearrange("p j c -> p (j c)"),
                 )
 

@@ -23,15 +23,23 @@ PASSES = D // K_PASS
 BANK = 512
 BANKS = D3 // BANK
 STORE_BANKS = 3
+W_LOAD_BANKS = 2
+QUADRANTS = 4
+QUADRANT = P // QUADRANTS
+SCALE_ROWS = 4
+BN_VALUES = 6
 EPS = 1e-6
 
-AHEAD_STATISTICS = 5
-AHEAD_NORMALISE = 3
-AHEAD_TRANSPOSE = 2
 AHEAD_QUANTISE = 1
-VECTOR_STATISTICS = 5
-VECTOR_REGROUPS = 2
-EARLY_X = 5
+AHEAD_TRANSPOSE = 2
+AHEAD_NORMALISE = 3
+AHEAD_STATISTICS = 5
+VECTOR_STATISTICS = AHEAD_STATISTICS
+VECTOR_REGROUPS = AHEAD_QUANTISE + 1
+EARLY_X = VECTOR_STATISTICS + 1
+
+TRANSPOSE_BANKS = 3
+PRODUCT_BANKS = 5
 
 FLOPS = 2 * P * SEQ * D * D3
 
@@ -46,8 +54,8 @@ def tile_timesformerlayer_pb_kernel(
         small = ctx.enter_context(tc.tile_pool(name="small", bufs=6))
         work = ctx.enter_context(tc.tile_pool(name="work", bufs=3))
         results = ctx.enter_context(tc.tile_pool(name="results", bufs=6))
-        psum_t = ctx.enter_context(tc.psum_pool(name="psum_t", bufs=3))
-        psum_a = ctx.enter_context(tc.psum_pool(name="psum_a", bufs=5))
+        psum_t = ctx.enter_context(tc.psum_pool(name="psum_t", bufs=TRANSPOSE_BANKS))
+        psum_a = ctx.enter_context(tc.psum_pool(name="psum_a", bufs=PRODUCT_BANKS))
         ctx.enter_context(tc.manual_schedule())
 
         bias_row = const.tile([P, D3], BF16)
@@ -84,13 +92,13 @@ def tile_timesformerlayer_pb_kernel(
 
         for s in range(EARLY_X):
             load_x(s)
-        for q in range(4):
+        for q in range(QUADRANTS):
             nc.sync.dma_start(
-                out=w_planes[32 * q : 32 * q + 4 * PASSES, :].bitcast(I32),
-                in_=s_qkv_w_scales[:, 4 * q : 4 * q + 4, :].bitcast(I32),
+                out=w_planes[QUADRANT * q : QUADRANT * q + SCALE_ROWS * PASSES, :].bitcast(I32),
+                in_=s_qkv_w_scales[:, SCALE_ROWS * q : SCALE_ROWS * (q + 1), :].bitcast(I32),
             )
         w_codes = const.tile([P, PASSES, D3], U32, align_bytes=64)
-        w_chunk = 2 * BANK
+        w_chunk = W_LOAD_BANKS * BANK
         for c in range(D3 // w_chunk):
             cols = slice(c * w_chunk, (c + 1) * w_chunk)
             for g in range(PASSES):
@@ -110,42 +118,52 @@ def tile_timesformerlayer_pb_kernel(
         nc.scalar.copy(out=gain_col[:], in_=gain_bf[:].rearrange("p g t -> p (g t)"))
         nc.scalar.copy(out=shift_col[:], in_=shift_bf[:].rearrange("p g t -> p (g t)"))
 
-        negmean, var_eps, xhat, planar, grouped, y_codes, y_planes = {}, {}, {}, {}, {}, {}, {}
+        negmean, var_eps, rstd, xhat, planar, grouped, y_codes, y_planes = {}, {}, {}, {}, {}, {}, {}, {}
 
-        def statistics(s):
-            negmean[s] = small.tile([P, 1], F32, tag="negmean", name="negmean%d" % s)
+        def vector_statistics(s):
+            parts = small.tile([P, PASSES, BN_VALUES], F32, tag="parts")
+            for h in range(PASSES):
+                nc.vector.bn_stats(out=parts[:, h, :], in_=x_sb[s][:, h * K_PASS : (h + 1) * K_PASS])
+            mean_var = small.tile([P, 2], F32, tag="mean_var")
+            nc.vector.bn_aggr(out=mean_var[:], in_=parts[:].rearrange("p h c -> p (h c)"))
             var_eps[s] = small.tile([P, 1], F32, tag="var_eps", name="var_eps%d" % s)
-            if s < VECTOR_STATISTICS:
-                parts = small.tile([P, PASSES, 6], F32, tag="parts")
-                for h in range(PASSES):
-                    nc.vector.bn_stats(out=parts[:, h, :], in_=x_sb[s][:, h * K_PASS : (h + 1) * K_PASS])
-                mean_var = small.tile([P, 2], F32, tag="mean_var")
-                nc.vector.bn_aggr(out=mean_var[:], in_=parts[:].rearrange("p h c -> p (h c)"))
-                nc.vector.tensor_scalar_add(out=var_eps[s][:], in0=mean_var[:, 1:2], scalar1=EPS)
-                nc.vector.tensor_scalar_mul(out=negmean[s][:], in0=mean_var[:, 0:1], scalar1=-1.0)
-            else:
-                rowsum = small.tile([P, 1], F32, tag="rowsum")
+            nc.vector.tensor_scalar_add(out=var_eps[s][:], in0=mean_var[:, 1:2], scalar1=EPS)
+            negmean[s] = small.tile([P, 1], F32, tag="negmean", name="negmean%d" % s)
+            nc.vector.tensor_scalar_mul(out=negmean[s][:], in0=mean_var[:, 0:1], scalar1=-1.0)
+
+        def scalar_mean(s):
+            negmean[s] = small.tile([P, 1], F32, tag="negmean", name="negmean%d" % s)
+            unread = work.tile([P, D], BF16, tag="unread", bufs=4)
+            nc.scalar.activation(
+                out=unread[:], in_=x_sb[s][:], func=ACT.Identity, scale=-1.0 / D, accum_out=negmean[s][:]
+            )
+
+        def scalar_statistics(s):
+            if VECTOR_STATISTICS <= s < SEQ:
                 sumsq = small.tile([P, 1], F32, tag="sumsq")
-                unread = work.tile([P, D], BF16, tag="unread", bufs=4)
-                nc.scalar.activation(out=unread[:], in_=x_sb[s][:], func=ACT.Identity, accum_out=rowsum[:])
-                nc.scalar.mul(negmean[s][:], rowsum[:], -1.0 / D)
                 unread = work.tile([P, D], BF16, tag="unread", bufs=4)
                 nc.scalar.activation(
                     out=unread[:], in_=x_sb[s][:], func=ACT.Square, bias=negmean[s][:], accum_out=sumsq[:]
                 )
+            if VECTOR_STATISTICS <= s + 1 < SEQ:
+                scalar_mean(s + 1)
+            if VECTOR_STATISTICS <= s < SEQ:
+                var_eps[s] = small.tile([P, 1], F32, tag="var_eps", name="var_eps%d" % s)
                 nc.scalar.activation(
                     out=var_eps[s][:], in_=sumsq[:], func=ACT.Identity, bias=eps_col[:], scale=1.0 / D
                 )
 
+        def reciprocal_std(s):
+            rstd[s] = small.tile([P, 1], F32, tag="rstd", name="rstd%d" % s)
+            nc.gpsimd.tensor_tensor(out=rstd[s][:], in0=var_eps[s][:], in1=minus_half[:], op=ALU.pow)
+
         def normalise(s):
-            rstd = small.tile([P, 1], F32, tag="rstd")
-            nc.gpsimd.tensor_tensor(out=rstd[:], in0=var_eps[s][:], in1=minus_half[:], op=ALU.pow)
             xhat[s] = work.tile([P, PASSES, PACK, P], F32, tag="xhat", name="xhat%d" % s, bufs=4)
             nc.gpsimd.tensor_scalar(
                 out=xhat[s][:],
                 in0=x_sb[s][:].rearrange("r (g p t) -> r g t p", g=PASSES, t=PACK),
                 scalar1=negmean[s][:],
-                scalar2=rstd[:],
+                scalar2=rstd[s][:],
                 op0=ALU.add,
                 op1=ALU.mult,
             )
@@ -186,10 +204,9 @@ def tile_timesformerlayer_pb_kernel(
             )
 
         def multiply(s):
-            store_banks = 1 if s == SEQ - 1 else STORE_BANKS
-            for first in range(0, BANKS, store_banks):
-                result = results.tile([P, store_banks, BANK], F32, tag="result")
-                for j in range(store_banks):
+            for first in range(0, BANKS, STORE_BANKS):
+                result = results.tile([P, STORE_BANKS, BANK], F32, tag="result")
+                for j in range(STORE_BANKS):
                     cols = slice((first + j) * BANK, (first + j + 1) * BANK)
                     acc = psum_a.tile([P, BANK], F32, tag="acc")
                     for g in range(PASSES):
@@ -198,24 +215,27 @@ def tile_timesformerlayer_pb_kernel(
                             lhsT=y_codes[s][:, g, :].bitcast(FP8X4),
                             lhsT_scale=y_planes[s][:, g, :],
                             rhs=w_codes[:, g, cols].bitcast(FP8X4),
-                            rhs_scale=w_planes[4 * g : P, cols],
+                            rhs_scale=w_planes[SCALE_ROWS * g : P, cols],
                             start=(g == 0),
                             stop=(g == PASSES - 1),
                         )
                     nc.vector.tensor_tensor(out=result[:, j, :], in0=acc[:], in1=bias_all[:, cols], op=ALU.add)
                 nc.sync.dma_start(
-                    out=out[:, s, first * BANK : (first + store_banks) * BANK],
+                    out=out[:, s, first * BANK : (first + STORE_BANKS) * BANK],
                     in_=result[:].rearrange("p j c -> p (j c)"),
                 )
 
         for s in range(-AHEAD_STATISTICS, SEQ):
             if 0 <= s + AHEAD_TRANSPOSE < SEQ:
                 transpose(s + AHEAD_TRANSPOSE)
+            if 0 <= s + AHEAD_NORMALISE < SEQ:
+                reciprocal_std(s + AHEAD_NORMALISE)
             if 0 <= s + AHEAD_QUANTISE < SEQ:
                 quantise(s + AHEAD_QUANTISE)
             if 0 <= s + AHEAD_NORMALISE < SEQ:
                 normalise(s + AHEAD_NORMALISE)
             if s >= 0:
                 multiply(s)
-            if s + AHEAD_STATISTICS < SEQ:
-                statistics(s + AHEAD_STATISTICS)
+            if s + AHEAD_STATISTICS < VECTOR_STATISTICS:
+                vector_statistics(s + AHEAD_STATISTICS)
+            scalar_statistics(s + AHEAD_STATISTICS)

@@ -23,7 +23,7 @@ PASSES = D // K_PASS
 BANK = 512
 BANKS = D3 // BANK
 STORE_BANKS = 3
-W_LOAD_BANKS = 2
+W_LOAD_BANKS = 3
 QUADRANTS = 4
 QUADRANT = P // QUADRANTS
 SCALE_ROWS = 4
@@ -36,6 +36,7 @@ AHEAD_NORMALISE = 3
 AHEAD_STATISTICS = 5
 VECTOR_STATISTICS = AHEAD_STATISTICS
 VECTOR_REGROUPS = AHEAD_QUANTISE + 1
+TILES_SHARING_W = BANKS // STORE_BANKS
 EARLY_X = VECTOR_STATISTICS + 1
 
 TRANSPOSE_BANKS = 3
@@ -203,29 +204,30 @@ def tile_timesformerlayer_pb_kernel(
                 in_=grouped[s][:].rearrange("p g r t -> p (g r t)"),
             )
 
-        def multiply(s):
-            for first in range(0, BANKS, STORE_BANKS):
-                result = results.tile([P, STORE_BANKS, BANK], F32, tag="result")
-                for j in range(STORE_BANKS):
-                    cols = slice((first + j) * BANK, (first + j + 1) * BANK)
-                    acc = psum_a.tile([P, BANK], F32, tag="acc")
-                    for g in range(PASSES):
-                        nc.tensor.matmul_mx(
-                            out=acc[:],
-                            lhsT=y_codes[s][:, g, :].bitcast(FP8X4),
-                            lhsT_scale=y_planes[s][:, g, :],
-                            rhs=w_codes[:, g, cols].bitcast(FP8X4),
-                            rhs_scale=w_planes[SCALE_ROWS * g : P, cols],
-                            start=(g == 0),
-                            stop=(g == PASSES - 1),
-                        )
-                    nc.vector.tensor_tensor(out=result[:, j, :], in0=acc[:], in1=bias_all[:, cols], op=ALU.add)
-                nc.sync.dma_start(
-                    out=out[:, s, first * BANK : (first + STORE_BANKS) * BANK],
-                    in_=result[:].rearrange("p j c -> p (j c)"),
-                )
+        def multiply(s, first):
+            result = results.tile([P, STORE_BANKS, BANK], F32, tag="result")
+            for j in range(STORE_BANKS):
+                cols = slice((first + j) * BANK, (first + j + 1) * BANK)
+                acc = psum_a.tile([P, BANK], F32, tag="acc")
+                for g in range(PASSES):
+                    nc.tensor.matmul_mx(
+                        out=acc[:],
+                        lhsT=y_codes[s][:, g, :].bitcast(FP8X4),
+                        lhsT_scale=y_planes[s][:, g, :],
+                        rhs=w_codes[:, g, cols].bitcast(FP8X4),
+                        rhs_scale=w_planes[SCALE_ROWS * g : P, cols],
+                        start=(g == 0),
+                        stop=(g == PASSES - 1),
+                    )
+                nc.vector.tensor_tensor(out=result[:, j, :], in0=acc[:], in1=bias_all[:, cols], op=ALU.add)
+            nc.sync.dma_start(
+                out=out[:, s, first * BANK : (first + STORE_BANKS) * BANK],
+                in_=result[:].rearrange("p j c -> p (j c)"),
+            )
 
         for s in range(-AHEAD_STATISTICS, SEQ):
+            if s + AHEAD_STATISTICS < VECTOR_STATISTICS:
+                vector_statistics(s + AHEAD_STATISTICS)
             if 0 <= s + AHEAD_TRANSPOSE < SEQ:
                 transpose(s + AHEAD_TRANSPOSE)
             if 0 <= s + AHEAD_NORMALISE < SEQ:
@@ -234,8 +236,10 @@ def tile_timesformerlayer_pb_kernel(
                 quantise(s + AHEAD_QUANTISE)
             if 0 <= s + AHEAD_NORMALISE < SEQ:
                 normalise(s + AHEAD_NORMALISE)
-            if s >= 0:
-                multiply(s)
-            if s + AHEAD_STATISTICS < VECTOR_STATISTICS:
-                vector_statistics(s + AHEAD_STATISTICS)
+            if 0 <= s < TILES_SHARING_W:
+                for tile in range(TILES_SHARING_W):
+                    multiply(tile, s * STORE_BANKS)
+            elif s >= 0:
+                for first in range(0, BANKS, STORE_BANKS):
+                    multiply(s, first)
             scalar_statistics(s + AHEAD_STATISTICS)

@@ -37,6 +37,7 @@ AHEAD_STATISTICS = 5
 VECTOR_STATISTICS = AHEAD_STATISTICS
 VECTOR_REGROUPS = AHEAD_QUANTISE + 1
 TILES_SHARING_W = BANKS // STORE_BANKS
+BIAS_AT_ONCE = BANKS // (AHEAD_TRANSPOSE + 1)
 EARLY_X = VECTOR_STATISTICS + 1
 
 TRANSPOSE_BANKS = 3
@@ -109,11 +110,13 @@ def tile_timesformerlayer_pb_kernel(
             load_x(s)
 
         bias_all = const.tile([P, D3], F32)
-        for j in range(BANKS):
+
+        def spread_bias(j):
             cols = slice(j * BANK, (j + 1) * BANK)
             acc = psum_a.tile([P, BANK], F32, tag="acc")
             nc.tensor.matmul(out=acc[:], lhsT=ones[:], rhs=bias_row[:, cols], start=True, stop=True)
             nc.scalar.copy(out=bias_all[:, cols], in_=acc[:])
+
         gain_col = const.tile([P, PASSES * PACK], F32)
         shift_col = const.tile([P, PASSES * PACK], F32)
         nc.scalar.copy(out=gain_col[:], in_=gain_bf[:].rearrange("p g t -> p (g t)"))
@@ -230,6 +233,10 @@ def tile_timesformerlayer_pb_kernel(
                 vector_statistics(s + AHEAD_STATISTICS)
             if 0 <= s + AHEAD_TRANSPOSE < SEQ:
                 transpose(s + AHEAD_TRANSPOSE)
+            before_run = s + AHEAD_TRANSPOSE + 1
+            if 0 <= before_run <= AHEAD_TRANSPOSE:
+                for j in range(BIAS_AT_ONCE * before_run, BIAS_AT_ONCE * (before_run + 1)):
+                    spread_bias(j)
             if 0 <= s + AHEAD_NORMALISE < SEQ:
                 reciprocal_std(s + AHEAD_NORMALISE)
             if 0 <= s + AHEAD_QUANTISE < SEQ:

@@ -109,13 +109,16 @@ def tile_timesformerlayer_pb_kernel(
         for s in range(EARLY_X, SEQ):
             load_x(s)
 
-        bias_all = const.tile([P, D3], F32)
+        bias_all = const.tile([P, D3], BF16)
 
-        def spread_bias(j):
-            cols = slice(j * BANK, (j + 1) * BANK)
-            acc = psum_a.tile([P, BANK], F32, tag="acc")
-            nc.tensor.matmul(out=acc[:], lhsT=ones[:], rhs=bias_row[:, cols], start=True, stop=True)
-            nc.scalar.copy(out=bias_all[:, cols], in_=acc[:])
+        def spread_bias(first):
+            spread = psum_a.tile([P, BIAS_AT_ONCE, BANK], BF16, tag="acc")
+            for h in range(BIAS_AT_ONCE):
+                cols = slice((first + h) * BANK, (first + h + 1) * BANK)
+                nc.tensor.matmul(out=spread[:, h, :], lhsT=ones[:], rhs=bias_row[:, cols], start=True, stop=True)
+            nc.scalar.copy(
+                out=bias_all[:, first * BANK : (first + BIAS_AT_ONCE) * BANK], in_=spread[:].rearrange("p h c -> p (h c)")
+            )
 
         gain_col = const.tile([P, PASSES * PACK], F32)
         shift_col = const.tile([P, PASSES * PACK], F32)
@@ -235,8 +238,7 @@ def tile_timesformerlayer_pb_kernel(
                 transpose(s + AHEAD_TRANSPOSE)
             before_run = s + AHEAD_TRANSPOSE + 1
             if 0 <= before_run <= AHEAD_TRANSPOSE:
-                for j in range(BIAS_AT_ONCE * before_run, BIAS_AT_ONCE * (before_run + 1)):
-                    spread_bias(j)
+                spread_bias(BIAS_AT_ONCE * before_run)
             if 0 <= s + AHEAD_NORMALISE < SEQ:
                 reciprocal_std(s + AHEAD_NORMALISE)
             if 0 <= s + AHEAD_QUANTISE < SEQ:

@@ -125,18 +125,34 @@ def tile_timesformerlayer_pb_kernel(
         nc.scalar.copy(out=gain_col[:], in_=gain_bf[:].rearrange("p g t -> p (g t)"))
         nc.scalar.copy(out=shift_col[:], in_=shift_bf[:].rearrange("p g t -> p (g t)"))
 
-        negmean, var_eps, rstd, xhat, planar, grouped, y_codes, y_planes = {}, {}, {}, {}, {}, {}, {}, {}
+        parts, mean_var, negmean, var_eps, rstd, xhat, planar, grouped, y_codes, y_planes = {}, {}, {}, {}, {}, {}, {}, {}, {}, {}
+
+        def half_sums(s, h):
+            if h == 0:
+                parts[s] = small.tile([P, PASSES, BN_VALUES], F32, tag="parts", name="parts%d" % s)
+            nc.vector.bn_stats(out=parts[s][:, h, :], in_=x_sb[s][:, h * K_PASS : (h + 1) * K_PASS])
+
+        def mean_and_variance(s):
+            mean_var[s] = small.tile([P, 2], F32, tag="mean_var", name="mean_var%d" % s)
+            nc.vector.bn_aggr(out=mean_var[s][:], in_=parts[s][:].rearrange("p h c -> p (h c)"))
+
+        def shifted(s):
+            var_eps[s] = small.tile([P, 1], F32, tag="var_eps", name="var_eps%d" % s)
+            nc.vector.tensor_scalar_add(out=var_eps[s][:], in0=mean_var[s][:, 1:2], scalar1=EPS)
+            negmean[s] = small.tile([P, 1], F32, tag="negmean", name="negmean%d" % s)
+            nc.vector.tensor_scalar_mul(out=negmean[s][:], in0=mean_var[s][:, 0:1], scalar1=-1.0)
 
         def vector_statistics(s):
-            parts = small.tile([P, PASSES, BN_VALUES], F32, tag="parts")
-            for h in range(PASSES):
-                nc.vector.bn_stats(out=parts[:, h, :], in_=x_sb[s][:, h * K_PASS : (h + 1) * K_PASS])
-            mean_var = small.tile([P, 2], F32, tag="mean_var")
-            nc.vector.bn_aggr(out=mean_var[:], in_=parts[:].rearrange("p h c -> p (h c)"))
-            var_eps[s] = small.tile([P, 1], F32, tag="var_eps", name="var_eps%d" % s)
-            nc.vector.tensor_scalar_add(out=var_eps[s][:], in0=mean_var[:, 1:2], scalar1=EPS)
-            negmean[s] = small.tile([P, 1], F32, tag="negmean", name="negmean%d" % s)
-            nc.vector.tensor_scalar_mul(out=negmean[s][:], in0=mean_var[:, 0:1], scalar1=-1.0)
+            woven = s - 1 if s > 1 else None
+            half_sums(s, 0)
+            if woven:
+                mean_and_variance(woven)
+            half_sums(s, 1)
+            if woven:
+                shifted(woven)
+            if s == 0 or s == VECTOR_STATISTICS - 1:
+                mean_and_variance(s)
+                shifted(s)
 
         def scalar_mean(s):
             negmean[s] = small.tile([P, 1], F32, tag="negmean", name="negmean%d" % s)

@@ -23,7 +23,6 @@ PASSES = D // K_PASS
 BANK = 512
 BANKS = D3 // BANK
 STORE_BANKS = 3
-W_LOAD_BANKS = 3
 QUADRANTS = 4
 QUADRANT = P // QUADRANTS
 SCALE_ROWS = 4
@@ -33,12 +32,12 @@ EPS = 1e-6
 AHEAD_QUANTISE = 1
 AHEAD_TRANSPOSE = 2
 AHEAD_NORMALISE = 3
-AHEAD_STATISTICS = 5
-VECTOR_STATISTICS = AHEAD_STATISTICS
-VECTOR_REGROUPS = AHEAD_QUANTISE + 1
-TILES_SHARING_W = BANKS // STORE_BANKS
-BIAS_AT_ONCE = BANKS // (AHEAD_TRANSPOSE + 1)
-EARLY_X = VECTOR_STATISTICS + 1
+AHEAD_STATISTICS = 4
+HEAD_TILES = 3
+VECTOR_REGROUPS = 2
+BIAS_AT_ONCE = 2
+SLOTS = 3
+EARLY_X = 3
 
 TRANSPOSE_BANKS = 3
 PRODUCT_BANKS = 5
@@ -60,6 +59,8 @@ def tile_timesformerlayer_pb_kernel(
         psum_a = ctx.enter_context(tc.psum_pool(name="psum_a", bufs=PRODUCT_BANKS))
         ctx.enter_context(tc.manual_schedule())
 
+        norm_rows = const.tile([P, K_PASS], BF16)
+        nc.vector.memset(norm_rows[:].bitcast(I32), 0)
         bias_row = const.tile([P, D3], BF16)
         nc.vector.memset(bias_row[:].bitcast(I32), 0)
         w_planes = const.tile([P, D3], U8, align_bytes=64)
@@ -73,11 +74,11 @@ def tile_timesformerlayer_pb_kernel(
         ident = const.tile([P, P], F32)
         make_identity(nc, ident[:])
 
-        gain_bf = const.tile([P, PASSES, PACK], BF16)
-        shift_bf = const.tile([P, PASSES, PACK], BF16)
+        nc.scalar.dma_start(out=norm_rows[0:PASSES, :], in_=ln1_g.rearrange("(g c) -> g c", g=PASSES))
+        nc.scalar.dma_start(out=norm_rows[PASSES : 2 * PASSES, :], in_=ln1_b.rearrange("(g c) -> g c", g=PASSES))
         nc.scalar.dma_start(out=bias_row[0:1, :], in_=s_qkv_b.unsqueeze(0))
-        nc.scalar.dma_start(out=gain_bf[:], in_=ln1_g.rearrange("(g p t) -> p g t", g=PASSES, p=P))
-        nc.scalar.dma_start(out=shift_bf[:], in_=ln1_b.rearrange("(g p t) -> p g t", g=PASSES, p=P))
+        ident_bf = const.tile([P, 2 * PASSES], BF16)
+        nc.gpsimd.tensor_copy(out=ident_bf[:], in_=ident[:, 0 : 2 * PASSES])
 
         x_sb = []
         for s in range(SEQ):
@@ -100,32 +101,53 @@ def tile_timesformerlayer_pb_kernel(
                 in_=s_qkv_w_scales[:, SCALE_ROWS * q : SCALE_ROWS * (q + 1), :].bitcast(I32),
             )
         w_codes = const.tile([P, PASSES, D3], U32, align_bytes=64)
-        w_chunk = W_LOAD_BANKS * BANK
-        for c in range(D3 // w_chunk):
-            cols = slice(c * w_chunk, (c + 1) * w_chunk)
+
+        def load_w(first, last):
+            cols = slice(first * BANK, last * BANK)
             for g in range(PASSES):
                 words = s_qkv_w_words[g].rearrange("p n t -> p (n t)").bitcast(I32)
                 nc.sync.dma_start(out=w_codes[:, g, cols].bitcast(I32), in_=words[:, cols])
-        for s in range(EARLY_X, SEQ):
+
+        load_w(0, 3)
+        load_x(3)
+        load_w(3, 4)
+        load_w(4, 6)
+        for s in range(4, SEQ):
             load_x(s)
 
         bias_all = const.tile([P, D3], BF16)
 
-        def spread_bias(first):
-            spread = psum_a.tile([P, BIAS_AT_ONCE, BANK], BF16, tag="acc")
+        spreads = {}
+
+        def spread_bias(i):
+            spreads[i] = psum_a.tile([P, BIAS_AT_ONCE, BANK], BF16, tag="acc", name="spread%d" % i)
             for h in range(BIAS_AT_ONCE):
-                cols = slice((first + h) * BANK, (first + h + 1) * BANK)
-                nc.tensor.matmul(out=spread[:, h, :], lhsT=ones[:], rhs=bias_row[:, cols], start=True, stop=True)
+                first = (BIAS_AT_ONCE * i + h) * BANK
+                nc.tensor.matmul(
+                    out=spreads[i][:, h, :], lhsT=ones[:], rhs=bias_row[:, first : first + BANK], start=True, stop=True
+                )
+
+        def copy_bias(i):
+            first = BIAS_AT_ONCE * i * BANK
             nc.scalar.copy(
-                out=bias_all[:, first * BANK : (first + BIAS_AT_ONCE) * BANK], in_=spread[:].rearrange("p h c -> p (h c)")
+                out=bias_all[:, first : first + BIAS_AT_ONCE * BANK], in_=spreads[i][:].rearrange("p h c -> p (h c)")
             )
 
-        gain_col = const.tile([P, PASSES * PACK], F32)
-        shift_col = const.tile([P, PASSES * PACK], F32)
-        nc.scalar.copy(out=gain_col[:], in_=gain_bf[:].rearrange("p g t -> p (g t)"))
-        nc.scalar.copy(out=shift_col[:], in_=shift_bf[:].rearrange("p g t -> p (g t)"))
+        norm_cols = const.tile([P, PACK, 2 * PASSES], F32)
 
-        parts, mean_var, negmean, var_eps, rstd, xhat, planar, grouped, y_codes, y_planes = {}, {}, {}, {}, {}, {}, {}, {}, {}, {}
+        def turn_norm_rows():
+            turned = psum_a.tile([P, PACK, 2 * PASSES], F32, tag="acc")
+            for t in range(PACK):
+                nc.tensor.matmul(
+                    out=turned[:, t, :], lhsT=norm_rows[:, t:K_PASS:PACK], rhs=ident_bf[:], start=True, stop=True
+                )
+            return turned
+
+        def copy_norm_cols(turned):
+            nc.scalar.copy(out=norm_cols[:], in_=turned[:])
+
+        parts, mean_var, negmean, sumsq, var_eps, rstd, xhat, planar, grouped = {}, {}, {}, {}, {}, {}, {}, {}, {}
+        y_codes, y_planes = {}, {}
 
         def half_sums(s, h):
             if h == 0:
@@ -136,23 +158,9 @@ def tile_timesformerlayer_pb_kernel(
             mean_var[s] = small.tile([P, 2], F32, tag="mean_var", name="mean_var%d" % s)
             nc.vector.bn_aggr(out=mean_var[s][:], in_=parts[s][:].rearrange("p h c -> p (h c)"))
 
-        def shifted(s):
+        def add_eps(s):
             var_eps[s] = small.tile([P, 1], F32, tag="var_eps", name="var_eps%d" % s)
             nc.vector.tensor_scalar_add(out=var_eps[s][:], in0=mean_var[s][:, 1:2], scalar1=EPS)
-            negmean[s] = small.tile([P, 1], F32, tag="negmean", name="negmean%d" % s)
-            nc.vector.tensor_scalar_mul(out=negmean[s][:], in0=mean_var[s][:, 0:1], scalar1=-1.0)
-
-        def vector_statistics(s):
-            woven = s - 1 if s > 1 else None
-            half_sums(s, 0)
-            if woven:
-                mean_and_variance(woven)
-            half_sums(s, 1)
-            if woven:
-                shifted(woven)
-            if s == 0 or s == VECTOR_STATISTICS - 1:
-                mean_and_variance(s)
-                shifted(s)
 
         def scalar_mean(s):
             negmean[s] = small.tile([P, 1], F32, tag="negmean", name="negmean%d" % s)
@@ -161,33 +169,41 @@ def tile_timesformerlayer_pb_kernel(
                 out=unread[:], in_=x_sb[s][:], func=ACT.Identity, scale=-1.0 / D, accum_out=negmean[s][:]
             )
 
+        def scalar_square(s):
+            sumsq[s] = small.tile([P, 1], F32, tag="sumsq", name="sumsq%d" % s)
+            unread = work.tile([P, D], BF16, tag="unread", bufs=4)
+            nc.scalar.activation(
+                out=unread[:], in_=x_sb[s][:], func=ACT.Square, bias=negmean[s][:], accum_out=sumsq[s][:]
+            )
+
+        def scalar_variance(s):
+            var_eps[s] = small.tile([P, 1], F32, tag="var_eps", name="var_eps%d" % s)
+            nc.scalar.activation(
+                out=var_eps[s][:], in_=sumsq[s][:], func=ACT.Identity, bias=eps_col[:], scale=1.0 / D
+            )
+
         def scalar_statistics(s):
-            if VECTOR_STATISTICS <= s < SEQ:
-                sumsq = small.tile([P, 1], F32, tag="sumsq")
-                unread = work.tile([P, D], BF16, tag="unread", bufs=4)
-                nc.scalar.activation(
-                    out=unread[:], in_=x_sb[s][:], func=ACT.Square, bias=negmean[s][:], accum_out=sumsq[:]
-                )
-            if VECTOR_STATISTICS <= s + 1 < SEQ:
+            if s < SEQ:
+                scalar_square(s)
+            if s + 1 < SEQ:
                 scalar_mean(s + 1)
-            if VECTOR_STATISTICS <= s < SEQ:
-                var_eps[s] = small.tile([P, 1], F32, tag="var_eps", name="var_eps%d" % s)
-                nc.scalar.activation(
-                    out=var_eps[s][:], in_=sumsq[:], func=ACT.Identity, bias=eps_col[:], scale=1.0 / D
-                )
+            if s < SEQ:
+                scalar_variance(s)
 
         def reciprocal_std(s):
             rstd[s] = small.tile([P, 1], F32, tag="rstd", name="rstd%d" % s)
             nc.gpsimd.tensor_tensor(out=rstd[s][:], in0=var_eps[s][:], in1=minus_half[:], op=ALU.pow)
 
         def normalise(s):
-            xhat[s] = work.tile([P, PASSES, PACK, P], F32, tag="xhat", name="xhat%d" % s, bufs=4)
-            nc.gpsimd.tensor_scalar(
+            xhat[s] = work.tile([P, PASSES, PACK, P], F32, tag="slot%d" % (s % SLOTS), name="xhat%d" % s, bufs=1, align_bytes=64)
+            engine = nc.vector if s < HEAD_TILES else nc.gpsimd
+            minus = s in mean_var
+            engine.tensor_scalar(
                 out=xhat[s][:],
                 in0=x_sb[s][:].rearrange("r (g p t) -> r g t p", g=PASSES, t=PACK),
-                scalar1=negmean[s][:],
+                scalar1=mean_var[s][:, 0:1] if minus else negmean[s][:],
                 scalar2=rstd[s][:],
-                op0=ALU.add,
+                op0=ALU.subtract if minus else ALU.add,
                 op1=ALU.mult,
             )
 
@@ -198,39 +214,46 @@ def tile_timesformerlayer_pb_kernel(
                 for t in range(PACK):
                     nc.tensor.transpose(out=bank[:, t, :], in_=xhat[s][:, g, t, :], identity=ident[:])
                 for t in range(PACK):
-                    c = g * PACK + t
                     nc.scalar.activation(
                         out=planar[s][:, g, t, :],
                         in_=bank[:, t, :],
                         func=ACT.Identity,
-                        scale=gain_col[:, c : c + 1],
-                        bias=shift_col[:, c : c + 1],
+                        scale=norm_cols[:, t, g : g + 1],
+                        bias=norm_cols[:, t, PASSES + g : PASSES + g + 1],
                     )
 
-        def quantise(s):
-            grouped[s] = work.tile([P, PASSES, P, PACK], BF16, tag="grouped", name="grouped%d" % s, align_bytes=64)
+        def regroup(s, g0, g1):
+            if g0 == 0:
+                grouped[s] = work.tile(
+                    [P, PASSES, P, PACK], BF16, tag="slot%d" % ((s + 2) % SLOTS), name="grouped%d" % s, bufs=1, align_bytes=64
+                )
             engine = nc.vector if s < VECTOR_REGROUPS else nc.gpsimd
             engine.tensor_scalar(
-                out=grouped[s][:],
-                in0=planar[s][:].rearrange("p g t r -> p g r t"),
+                out=grouped[s][:, g0:g1],
+                in0=planar[s][:, g0:g1].rearrange("p g t r -> p g r t"),
                 scalar1=1.0,
                 scalar2=0.0,
                 op0=ALU.mult,
                 op1=ALU.add,
             )
-            y_codes[s] = const.tile([P, PASSES, P], U32, name="y_codes%d" % s, align_bytes=64)
-            y_planes[s] = const.tile([P, PASSES, P], U8, name="y_planes%d" % s, align_bytes=64)
+
+        def quantise(s, g0, g1):
+            if g0 == 0:
+                y_codes[s] = const.tile([P, PASSES, P], U32, name="y_codes%d" % s, align_bytes=64)
+                y_planes[s] = const.tile([P, PASSES, P], U8, name="y_planes%d" % s, align_bytes=64)
             nc.vector.quantize_mx(
-                out=y_codes[s][:].rearrange("p g r -> p (g r)").bitcast(FP8X4),
-                scales=y_planes[s][:].rearrange("p g r -> p (g r)"),
-                in_=grouped[s][:].rearrange("p g r t -> p (g r t)"),
+                out=y_codes[s][:, g0:g1].rearrange("p g r -> p (g r)").bitcast(FP8X4),
+                scales=y_planes[s][:, g0:g1].rearrange("p g r -> p (g r)"),
+                in_=grouped[s][:, g0:g1].rearrange("p g r t -> p (g r t)"),
             )
 
-        def multiply(s, first):
-            result = results.tile([P, STORE_BANKS, BANK], F32, tag="result")
-            for j in range(STORE_BANKS):
-                cols = slice((first + j) * BANK, (first + j + 1) * BANK)
-                acc = psum_a.tile([P, BANK], F32, tag="acc")
+        accs, results_of = {}, {}
+
+        def passes(s, first):
+            for j in range(first, first + STORE_BANKS):
+                cols = slice(j * BANK, (j + 1) * BANK)
+                acc = psum_a.tile([P, BANK], F32, tag="acc", name="acc%d_%d" % (s, j))
+                accs[s, j] = acc
                 for g in range(PASSES):
                     nc.tensor.matmul_mx(
                         out=acc[:],
@@ -241,30 +264,95 @@ def tile_timesformerlayer_pb_kernel(
                         start=(g == 0),
                         stop=(g == PASSES - 1),
                     )
-                nc.vector.tensor_tensor(out=result[:, j, :], in0=acc[:], in1=bias_all[:, cols], op=ALU.add)
-            nc.sync.dma_start(
-                out=out[:, s, first * BANK : (first + STORE_BANKS) * BANK],
-                in_=result[:].rearrange("p j c -> p (j c)"),
-            )
 
-        for s in range(-AHEAD_STATISTICS, SEQ):
-            if s + AHEAD_STATISTICS < VECTOR_STATISTICS:
-                vector_statistics(s + AHEAD_STATISTICS)
-            if 0 <= s + AHEAD_TRANSPOSE < SEQ:
+        def empty(s, j):
+            cols = slice(j * BANK, (j + 1) * BANK)
+            half, slot = divmod(j, STORE_BANKS)
+            if slot == 0:
+                result = results.tile([P, STORE_BANKS, BANK], F32, tag="result", name="result%d_%d" % (s, half))
+                results_of[s, half] = result
+            result = results_of[s, half]
+            nc.vector.tensor_tensor(out=result[:, slot, :], in0=accs[s, j][:], in1=bias_all[:, cols], op=ALU.add)
+            if slot == STORE_BANKS - 1:
+                nc.sync.dma_start(
+                    out=out[:, s, half * STORE_BANKS * BANK : (half + 1) * STORE_BANKS * BANK],
+                    in_=result[:].rearrange("p j c -> p (j c)"),
+                )
+
+        def multiply(s, first):
+            passes(s, first)
+            for j in range(first, first + STORE_BANKS):
+                empty(s, j)
+
+        turned = turn_norm_rows()
+        spread_bias(0)
+        half_sums(0, 0)
+        half_sums(0, 1)
+        scalar_mean(1)
+        copy_norm_cols(turned)
+        mean_and_variance(0)
+        add_eps(0)
+        reciprocal_std(0)
+        half_sums(2, 0)
+        normalise(0)
+        scalar_square(1)
+        scalar_variance(1)
+        reciprocal_std(1)
+        transpose(0)
+        copy_bias(0)
+        spread_bias(1)
+        spread_bias(2)
+        half_sums(2, 1)
+        mean_and_variance(2)
+        add_eps(2)
+        reciprocal_std(2)
+        normalise(1)
+        regroup(0, 0, 1)
+        transpose(1)
+        regroup(0, 1, 2)
+        quantise(0, 0, 1)
+        quantise(0, 1, 2)
+        copy_bias(1)
+        normalise(2)
+        passes(0, 0)
+        regroup(1, 0, 2)
+        empty(0, 0)
+        quantise(1, 0, 2)
+        empty(0, 1)
+        empty(0, 2)
+        scalar_mean(3)
+        copy_bias(2)
+        scalar_square(3)
+        scalar_variance(3)
+        transpose(2)
+        multiply(1, 0)
+        scalar_mean(4)
+        scalar_statistics(4)
+        reciprocal_std(3)
+        normalise(3)
+        regroup(2, 0, PASSES)
+        multiply(0, STORE_BANKS)
+        quantise(2, 0, PASSES)
+        transpose(3)
+        scalar_statistics(5)
+        reciprocal_std(4)
+        normalise(4)
+        regroup(3, 0, PASSES)
+        multiply(1, STORE_BANKS)
+
+        for s in range(2, SEQ):
+            multiply(s, 0)
+            if s + AHEAD_QUANTISE < SEQ:
+                quantise(s + AHEAD_QUANTISE, 0, PASSES)
+            if s < 3:
+                multiply(s, STORE_BANKS)
+            if s + AHEAD_TRANSPOSE < SEQ:
                 transpose(s + AHEAD_TRANSPOSE)
-            before_run = s + AHEAD_TRANSPOSE + 1
-            if 0 <= before_run <= AHEAD_TRANSPOSE:
-                spread_bias(BIAS_AT_ONCE * before_run)
-            if 0 <= s + AHEAD_NORMALISE < SEQ:
-                reciprocal_std(s + AHEAD_NORMALISE)
-            if 0 <= s + AHEAD_QUANTISE < SEQ:
-                quantise(s + AHEAD_QUANTISE)
-            if 0 <= s + AHEAD_NORMALISE < SEQ:
-                normalise(s + AHEAD_NORMALISE)
-            if 0 <= s < TILES_SHARING_W:
-                for tile in range(TILES_SHARING_W):
-                    multiply(tile, s * STORE_BANKS)
-            elif s >= 0:
-                for first in range(0, BANKS, STORE_BANKS):
-                    multiply(s, first)
             scalar_statistics(s + AHEAD_STATISTICS)
+            if s + AHEAD_NORMALISE < SEQ:
+                reciprocal_std(s + AHEAD_NORMALISE)
+                normalise(s + AHEAD_NORMALISE)
+            if s + AHEAD_TRANSPOSE < SEQ:
+                regroup(s + AHEAD_TRANSPOSE, 0, PASSES)
+            if s >= 3:
+                multiply(s, STORE_BANKS)

@@ -129,9 +129,8 @@ def tile_timesformerlayer_pb_kernel(
 
         def copy_bias(i):
             first = BIAS_AT_ONCE * i * BANK
-            nc.scalar.copy(
-                out=bias_all[:, first : first + BIAS_AT_ONCE * BANK], in_=spreads[i][:].rearrange("p h c -> p (h c)")
-            )
+            copy = nc.vector.tensor_copy if i == 2 else nc.scalar.copy
+            copy(out=bias_all[:, first : first + BIAS_AT_ONCE * BANK], in_=spreads[i][:].rearrange("p h c -> p (h c)"))
 
         norm_cols = const.tile([P, PACK, 2 * PASSES], F32)
 
@@ -161,6 +160,9 @@ def tile_timesformerlayer_pb_kernel(
         def add_eps(s):
             var_eps[s] = small.tile([P, 1], F32, tag="var_eps", name="var_eps%d" % s)
             nc.vector.tensor_scalar_add(out=var_eps[s][:], in0=mean_var[s][:, 1:2], scalar1=EPS)
+            if s >= HEAD_TILES:
+                negmean[s] = small.tile([P, 1], F32, tag="negmean", name="negmean%d" % s)
+                nc.vector.tensor_scalar_mul(out=negmean[s][:], in0=mean_var[s][:, 0:1], scalar1=-1.0)
 
         def scalar_mean(s):
             negmean[s] = small.tile([P, 1], F32, tag="negmean", name="negmean%d" % s)
@@ -197,7 +199,7 @@ def tile_timesformerlayer_pb_kernel(
         def normalise(s):
             xhat[s] = work.tile([P, PASSES, PACK, P], F32, tag="slot%d" % (s % SLOTS), name="xhat%d" % s, bufs=1, align_bytes=64)
             engine = nc.vector if s < HEAD_TILES else nc.gpsimd
-            minus = s in mean_var
+            minus = s not in negmean
             engine.tensor_scalar(
                 out=xhat[s][:],
                 in0=x_sb[s][:].rearrange("r (g p t) -> r g t p", g=PASSES, t=PACK),
@@ -273,7 +275,9 @@ def tile_timesformerlayer_pb_kernel(
                 results_of[s, half] = result
             result = results_of[s, half]
             nc.vector.tensor_tensor(out=result[:, slot, :], in0=accs[s, j][:], in1=bias_all[:, cols], op=ALU.add)
-            if slot == STORE_BANKS - 1:
+            if s >= SEQ - 3:
+                nc.sync.dma_start(out=out[:, s, cols], in_=result[:, slot, :])
+            elif slot == STORE_BANKS - 1:
                 nc.sync.dma_start(
                     out=out[:, s, half * STORE_BANKS * BANK : (half + 1) * STORE_BANKS * BANK],
                     in_=result[:].rearrange("p j c -> p (j c)"),
@@ -316,29 +320,35 @@ def tile_timesformerlayer_pb_kernel(
         normalise(2)
         passes(0, 0)
         regroup(1, 0, 2)
-        empty(0, 0)
+        copy_bias(2)
         quantise(1, 0, 2)
+        empty(0, 0)
         empty(0, 1)
         empty(0, 2)
         scalar_mean(3)
-        copy_bias(2)
         scalar_square(3)
         scalar_variance(3)
         transpose(2)
         multiply(1, 0)
-        scalar_mean(4)
-        scalar_statistics(4)
         reciprocal_std(3)
         normalise(3)
         regroup(2, 0, PASSES)
         multiply(0, STORE_BANKS)
+        half_sums(4, 0)
         quantise(2, 0, PASSES)
+        half_sums(4, 1)
+        mean_and_variance(4)
+        scalar_mean(5)
         transpose(3)
+        passes(1, STORE_BANKS)
+        empty(1, STORE_BANKS)
+        add_eps(4)
+        empty(1, STORE_BANKS + 1)
+        empty(1, STORE_BANKS + 2)
         scalar_statistics(5)
+        regroup(3, 0, PASSES)
         reciprocal_std(4)
         normalise(4)
-        regroup(3, 0, PASSES)
-        multiply(1, STORE_BANKS)
 
         for s in range(2, SEQ):
             multiply(s, 0)

@@ -74,9 +74,6 @@ def tile_timesformerlayer_pb_kernel(
         ident = const.tile([P, P], F32)
         make_identity(nc, ident[:])
 
-        nc.scalar.dma_start(out=norm_rows[0:PASSES, :], in_=ln1_g.rearrange("(g c) -> g c", g=PASSES))
-        nc.scalar.dma_start(out=norm_rows[PASSES : 2 * PASSES, :], in_=ln1_b.rearrange("(g c) -> g c", g=PASSES))
-        nc.scalar.dma_start(out=bias_row[0:1, :], in_=s_qkv_b.unsqueeze(0))
         ident_bf = const.tile([P, 2 * PASSES], BF16)
         nc.gpsimd.tensor_copy(out=ident_bf[:], in_=ident[:, 0 : 2 * PASSES])
 
@@ -93,26 +90,42 @@ def tile_timesformerlayer_pb_kernel(
                 rows = x_res[:, first : first + FRAMES, :]
             nc.sync.dma_start(out=x_sb[s][:], in_=rows)
 
-        for s in range(EARLY_X):
-            load_x(s)
-        for q in range(QUADRANTS):
-            nc.sync.dma_start(
-                out=w_planes[QUADRANT * q : QUADRANT * q + SCALE_ROWS * PASSES, :].bitcast(I32),
-                in_=s_qkv_w_scales[:, SCALE_ROWS * q : SCALE_ROWS * (q + 1), :].bitcast(I32),
-            )
+        def load_norm_rows():
+            nc.scalar.dma_start(out=norm_rows[0:PASSES, :], in_=ln1_g.rearrange("(g c) -> g c", g=PASSES))
+            nc.scalar.dma_start(out=norm_rows[PASSES : 2 * PASSES, :], in_=ln1_b.rearrange("(g c) -> g c", g=PASSES))
+
+        def load_bias():
+            nc.scalar.dma_start(out=bias_row[0:1, :], in_=s_qkv_b.unsqueeze(0))
+
+        def load_scales():
+            for q in range(QUADRANTS):
+                nc.sync.dma_start(
+                    out=w_planes[QUADRANT * q : QUADRANT * q + SCALE_ROWS * PASSES, :].bitcast(I32),
+                    in_=s_qkv_w_scales[:, SCALE_ROWS * q : SCALE_ROWS * (q + 1), :].bitcast(I32),
+                )
+
         w_codes = const.tile([P, PASSES, D3], U32, align_bytes=64)
 
-        def load_w(first, last):
+        def load_w(g, first, last):
+            words = s_qkv_w_words[g].rearrange("p n t -> p (n t)").bitcast(I32)
             cols = slice(first * BANK, last * BANK)
-            for g in range(PASSES):
-                words = s_qkv_w_words[g].rearrange("p n t -> p (n t)").bitcast(I32)
-                nc.sync.dma_start(out=w_codes[:, g, cols].bitcast(I32), in_=words[:, cols])
+            nc.sync.dma_start(out=w_codes[:, g, cols].bitcast(I32), in_=words[:, cols])
 
-        load_w(0, 3)
+        load_x(0)
+        load_x(1)
+        load_norm_rows()
+        load_bias()
+        load_x(2)
+        load_w(0, 0, 3)
+        load_scales()
+        load_w(1, 0, 3)
         load_x(3)
-        load_w(3, 4)
-        load_w(4, 6)
-        for s in range(4, SEQ):
+        load_w(0, 3, 4)
+        load_w(1, 3, 4)
+        load_x(4)
+        load_w(0, 4, 6)
+        load_w(1, 4, 6)
+        for s in range(5, SEQ):
             load_x(s)
 
         bias_all = const.tile([P, D3], BF16)
@@ -129,8 +142,7 @@ def tile_timesformerlayer_pb_kernel(
 
         def copy_bias(i):
             first = BIAS_AT_ONCE * i * BANK
-            copy = nc.vector.tensor_copy if i == 2 else nc.scalar.copy
-            copy(out=bias_all[:, first : first + BIAS_AT_ONCE * BANK], in_=spreads[i][:].rearrange("p h c -> p (h c)"))
+            nc.scalar.copy(out=bias_all[:, first : first + BIAS_AT_ONCE * BANK], in_=spreads[i][:].rearrange("p h c -> p (h c)"))
 
         norm_cols = const.tile([P, PACK, 2 * PASSES], F32)
 
@@ -251,21 +263,22 @@ def tile_timesformerlayer_pb_kernel(
 
         accs, results_of = {}, {}
 
-        def passes(s, first):
-            for j in range(first, first + STORE_BANKS):
+        def passes(s, first, by_pass=False):
+            js = range(first, first + STORE_BANKS)
+            for j in js:
+                accs[s, j] = psum_a.tile([P, BANK], F32, tag="acc", name="acc%d_%d" % (s, j))
+            order = [(j, g) for g in range(PASSES) for j in js] if by_pass else [(j, g) for j in js for g in range(PASSES)]
+            for j, g in order:
                 cols = slice(j * BANK, (j + 1) * BANK)
-                acc = psum_a.tile([P, BANK], F32, tag="acc", name="acc%d_%d" % (s, j))
-                accs[s, j] = acc
-                for g in range(PASSES):
-                    nc.tensor.matmul_mx(
-                        out=acc[:],
-                        lhsT=y_codes[s][:, g, :].bitcast(FP8X4),
-                        lhsT_scale=y_planes[s][:, g, :],
-                        rhs=w_codes[:, g, cols].bitcast(FP8X4),
-                        rhs_scale=w_planes[SCALE_ROWS * g : P, cols],
-                        start=(g == 0),
-                        stop=(g == PASSES - 1),
-                    )
+                nc.tensor.matmul_mx(
+                    out=accs[s, j][:],
+                    lhsT=y_codes[s][:, g, :].bitcast(FP8X4),
+                    lhsT_scale=y_planes[s][:, g, :],
+                    rhs=w_codes[:, g, cols].bitcast(FP8X4),
+                    rhs_scale=w_planes[SCALE_ROWS * g : P, cols],
+                    start=(g == 0),
+                    stop=(g == PASSES - 1),
+                )
 
         def empty(s, j):
             cols = slice(j * BANK, (j + 1) * BANK)
@@ -275,9 +288,7 @@ def tile_timesformerlayer_pb_kernel(
                 results_of[s, half] = result
             result = results_of[s, half]
             nc.vector.tensor_tensor(out=result[:, slot, :], in0=accs[s, j][:], in1=bias_all[:, cols], op=ALU.add)
-            if s >= SEQ - 3:
-                nc.sync.dma_start(out=out[:, s, cols], in_=result[:, slot, :])
-            elif slot == STORE_BANKS - 1:
+            if slot == STORE_BANKS - 1:
                 nc.sync.dma_start(
                     out=out[:, s, half * STORE_BANKS * BANK : (half + 1) * STORE_BANKS * BANK],
                     in_=result[:].rearrange("p j c -> p (j c)"),
@@ -316,39 +327,46 @@ def tile_timesformerlayer_pb_kernel(
         regroup(0, 1, 2)
         quantise(0, 0, 1)
         quantise(0, 1, 2)
+        copy_bias(2)
         copy_bias(1)
         normalise(2)
-        passes(0, 0)
-        regroup(1, 0, 2)
-        copy_bias(2)
-        quantise(1, 0, 2)
+        passes(0, 0, by_pass=True)
+        regroup(1, 0, 1)
+        regroup(1, 1, 2)
+        quantise(1, 0, 1)
         empty(0, 0)
+        quantise(1, 1, 2)
+        half_sums(3, 0)
         empty(0, 1)
+        half_sums(3, 1)
         empty(0, 2)
-        scalar_mean(3)
-        scalar_square(3)
-        scalar_variance(3)
+        mean_and_variance(3)
         transpose(2)
-        multiply(1, 0)
+        passes(1, 0, by_pass=True)
+        empty(1, 0)
+        add_eps(3)
+        empty(1, 1)
+        empty(1, 2)
+        scalar_mean(4)
+        scalar_square(4)
+        scalar_variance(4)
+        scalar_mean(5)
+        regroup(2, 0, PASSES)
         reciprocal_std(3)
         normalise(3)
-        regroup(2, 0, PASSES)
-        multiply(0, STORE_BANKS)
-        half_sums(4, 0)
+        passes(0, STORE_BANKS)
+        empty(0, 3)
         quantise(2, 0, PASSES)
-        half_sums(4, 1)
-        mean_and_variance(4)
-        scalar_mean(5)
-        transpose(3)
+        empty(0, 4)
+        empty(0, 5)
         passes(1, STORE_BANKS)
-        empty(1, STORE_BANKS)
-        add_eps(4)
-        empty(1, STORE_BANKS + 1)
-        empty(1, STORE_BANKS + 2)
+        transpose(3)
+        for j in range(3, 6):
+            empty(1, j)
         scalar_statistics(5)
-        regroup(3, 0, PASSES)
         reciprocal_std(4)
         normalise(4)
+        regroup(3, 0, PASSES)
 
         for s in range(2, SEQ):
             multiply(s, 0)

@@ -74,6 +74,9 @@ def tile_timesformerlayer_pb_kernel(
         ident = const.tile([P, P], F32)
         make_identity(nc, ident[:])
 
+        nc.scalar.dma_start(out=norm_rows[0:PASSES, :], in_=ln1_g.rearrange("(g c) -> g c", g=PASSES))
+        nc.scalar.dma_start(out=norm_rows[PASSES : 2 * PASSES, :], in_=ln1_b.rearrange("(g c) -> g c", g=PASSES))
+        nc.scalar.dma_start(out=bias_row[0:1, :], in_=s_qkv_b.unsqueeze(0))
         ident_bf = const.tile([P, 2 * PASSES], BF16)
         nc.gpsimd.tensor_copy(out=ident_bf[:], in_=ident[:, 0 : 2 * PASSES])
 
@@ -90,41 +93,26 @@ def tile_timesformerlayer_pb_kernel(
                 rows = x_res[:, first : first + FRAMES, :]
             nc.sync.dma_start(out=x_sb[s][:], in_=rows)
 
-        def load_norm_rows():
-            nc.scalar.dma_start(out=norm_rows[0:PASSES, :], in_=ln1_g.rearrange("(g c) -> g c", g=PASSES))
-            nc.scalar.dma_start(out=norm_rows[PASSES : 2 * PASSES, :], in_=ln1_b.rearrange("(g c) -> g c", g=PASSES))
-
-        def load_bias():
-            nc.scalar.dma_start(out=bias_row[0:1, :], in_=s_qkv_b.unsqueeze(0))
-
-        def load_scales():
-            for q in range(QUADRANTS):
-                nc.sync.dma_start(
-                    out=w_planes[QUADRANT * q : QUADRANT * q + SCALE_ROWS * PASSES, :].bitcast(I32),
-                    in_=s_qkv_w_scales[:, SCALE_ROWS * q : SCALE_ROWS * (q + 1), :].bitcast(I32),
-                )
-
+        for s in range(EARLY_X):
+            load_x(s)
+        for q in range(QUADRANTS):
+            nc.sync.dma_start(
+                out=w_planes[QUADRANT * q : QUADRANT * q + SCALE_ROWS * PASSES, :].bitcast(I32),
+                in_=s_qkv_w_scales[:, SCALE_ROWS * q : SCALE_ROWS * (q + 1), :].bitcast(I32),
+            )
         w_codes = const.tile([P, PASSES, D3], U32, align_bytes=64)
 
-        def load_w(g, first, last):
-            words = s_qkv_w_words[g].rearrange("p n t -> p (n t)").bitcast(I32)
+        def load_w(first, last):
             cols = slice(first * BANK, last * BANK)
-            nc.sync.dma_start(out=w_codes[:, g, cols].bitcast(I32), in_=words[:, cols])
+            for g in range(PASSES):
+                words = s_qkv_w_words[g].rearrange("p n t -> p (n t)").bitcast(I32)
+                nc.sync.dma_start(out=w_codes[:, g, cols].bitcast(I32), in_=words[:, cols])
 
-        load_x(0)
-        load_x(1)
-        load_norm_rows()
-        load_bias()
-        load_x(2)
-        load_w(0, 0, 3)
-        load_scales()
-        load_w(1, 0, 3)
+        load_w(0, 3)
         load_x(3)
-        load_w(0, 3, 4)
-        load_w(1, 3, 4)
         load_x(4)
-        load_w(0, 4, 6)
-        load_w(1, 4, 6)
+        load_w(3, 4)
+        load_w(4, 6)
         for s in range(5, SEQ):
             load_x(s)
 
@@ -288,7 +276,9 @@ def tile_timesformerlayer_pb_kernel(
                 results_of[s, half] = result
             result = results_of[s, half]
             nc.vector.tensor_tensor(out=result[:, slot, :], in0=accs[s, j][:], in1=bias_all[:, cols], op=ALU.add)
-            if slot == STORE_BANKS - 1:
+            if s >= SEQ - 3:
+                nc.sync.dma_start(out=out[:, s, cols], in_=result[:, slot, :])
+            elif slot == STORE_BANKS - 1:
                 nc.sync.dma_start(
                     out=out[:, s, half * STORE_BANKS * BANK : (half + 1) * STORE_BANKS * BANK],
                     in_=result[:].rearrange("p j c -> p (j c)"),

@@ -85,11 +85,14 @@ def tile_timesformerlayer_pb_kernel(
             x_tile = const.tile([P, D], BF16, name="x%d" % s)
             x_sb.append(x_tile)
 
+        def position(s):
+            return (s + 1) % SEQ
+
         def load_x(s):
-            if s == 0:
+            if position(s) == 0:
                 rows = x_res[:, 0:1, :].to_broadcast([SAMPLES, FRAMES, D])
             else:
-                first = 1 + (s - 1) * FRAMES
+                first = 1 + (position(s) - 1) * FRAMES
                 rows = x_res[:, first : first + FRAMES, :]
             nc.sync.dma_start(out=x_sb[s][:], in_=rows)
 
@@ -277,10 +280,10 @@ def tile_timesformerlayer_pb_kernel(
             result = results_of[s, half]
             nc.vector.tensor_tensor(out=result[:, slot, :], in0=accs[s, j][:], in1=bias_all[:, cols], op=ALU.add)
             if s >= SEQ - 3:
-                nc.sync.dma_start(out=out[:, s, cols], in_=result[:, slot, :])
+                nc.sync.dma_start(out=out[:, position(s), cols], in_=result[:, slot, :])
             elif slot == STORE_BANKS - 1:
                 nc.sync.dma_start(
-                    out=out[:, s, half * STORE_BANKS * BANK : (half + 1) * STORE_BANKS * BANK],
+                    out=out[:, position(s), half * STORE_BANKS * BANK : (half + 1) * STORE_BANKS * BANK],
                     in_=result[:].rearrange("p j c -> p (j c)"),
                 )
 

@@ -113,8 +113,8 @@ def tile_timesformerlayer_pb_kernel(
 
         load_w(0, 3)
         load_x(3)
-        load_x(4)
         load_w(3, 4)
+        load_x(4)
         load_w(4, 6)
         for s in range(5, SEQ):
             load_x(s)
@@ -254,8 +254,8 @@ def tile_timesformerlayer_pb_kernel(
 
         accs, results_of = {}, {}
 
-        def passes(s, first, by_pass=False):
-            js = range(first, first + STORE_BANKS)
+        def passes(s, first, banks=STORE_BANKS, by_pass=False):
+            js = range(first, first + banks)
             for j in js:
                 accs[s, j] = psum_a.tile([P, BANK], F32, tag="acc", name="acc%d_%d" % (s, j))
             order = [(j, g) for g in range(PASSES) for j in js] if by_pass else [(j, g) for j in js for g in range(PASSES)]
@@ -347,15 +347,13 @@ def tile_timesformerlayer_pb_kernel(
         regroup(2, 0, PASSES)
         reciprocal_std(3)
         normalise(3)
-        passes(0, STORE_BANKS)
-        empty(0, 3)
-        quantise(2, 0, PASSES)
-        empty(0, 4)
-        empty(0, 5)
-        passes(1, STORE_BANKS)
+        for j in range(STORE_BANKS, BANKS):
+            for tile in range(2):
+                passes(tile, j, 1)
+                empty(tile, j)
+            if j == STORE_BANKS:
+                quantise(2, 0, PASSES)
         transpose(3)
-        for j in range(3, 6):
-            empty(1, j)
         scalar_statistics(5)
         reciprocal_std(4)
         normalise(4)

@@ -294,6 +294,7 @@ def tile_timesformerlayer_pb_kernel(
 
         turned = turn_norm_rows()
         spread_bias(0)
+        spread_bias(1)
         half_sums(0, 0)
         half_sums(0, 1)
         scalar_mean(1)
@@ -308,7 +309,6 @@ def tile_timesformerlayer_pb_kernel(
         reciprocal_std(1)
         transpose(0)
         copy_bias(0)
-        spread_bias(1)
         spread_bias(2)
         half_sums(2, 1)
         mean_and_variance(2)

from contextlib import ExitStack

import concourse.mybir as mybir
from concourse.masks import make_identity

F32 = mybir.dt.float32
BF16 = mybir.dt.bfloat16
U8 = mybir.dt.uint8
U32 = mybir.dt.uint32
I32 = mybir.dt.int32
FP8X4 = mybir.dt.float8_e4m3fn_x4
ALU = mybir.AluOpType
ACT = mybir.ActivationFunctionType

P = 128
SAMPLES, FRAMES, PATCHES = 16, 8, 12
SEQ = 1 + PATCHES
D = 1024
D3 = 3072
PACK = 4
K_PASS = P * PACK
PASSES = D // K_PASS
BANK = 512
BANKS = D3 // BANK
STORE_BANKS = 3
QUADRANTS = 4
QUADRANT = P // QUADRANTS
SCALE_ROWS = 4
BN_VALUES = 6
EPS = 1e-6

AHEAD_QUANTISE = 1
AHEAD_TRANSPOSE = 2
AHEAD_NORMALISE = 3
AHEAD_STATISTICS = 4
HEAD_TILES = 3
VECTOR_REGROUPS = 2
BIAS_AT_ONCE = 2
SLOTS = 3
EARLY_X = 3

TRANSPOSE_BANKS = 3
PRODUCT_BANKS = 5

FLOPS = 2 * P * SEQ * D * D3


def tile_timesformerlayer_pb_kernel(
    tc, x_res, ln1_g, ln1_b, s_qkv_w_words, s_qkv_w_scales, s_qkv_b, out
):
    nc = tc.nc

    with ExitStack() as ctx:
        const = ctx.enter_context(tc.tile_pool(name="const", bufs=1))
        small = ctx.enter_context(tc.tile_pool(name="small", bufs=6))
        work = ctx.enter_context(tc.tile_pool(name="work", bufs=3))
        results = ctx.enter_context(tc.tile_pool(name="results", bufs=6))
        psum_t = ctx.enter_context(tc.psum_pool(name="psum_t", bufs=TRANSPOSE_BANKS))
        psum_a = ctx.enter_context(tc.psum_pool(name="psum_a", bufs=PRODUCT_BANKS))
        ctx.enter_context(tc.manual_schedule())

        norm_rows = const.tile([P, K_PASS], BF16)
        nc.vector.memset(norm_rows[:].bitcast(I32), 0)
        bias_row = const.tile([P, D3], BF16)
        nc.vector.memset(bias_row[:].bitcast(I32), 0)
        w_planes = const.tile([P, D3], U8, align_bytes=64)
        nc.vector.memset(w_planes[:].bitcast(I32), 0)
        ones = const.tile([P, P], BF16)
        nc.vector.memset(ones[:], 1.0)
        eps_col = const.tile([P, 1], F32)
        nc.vector.memset(eps_col[:], EPS)
        minus_half = const.tile([P, 1], F32)
        nc.vector.memset(minus_half[:], -0.5)
        ident = const.tile([P, P], F32)
        make_identity(nc, ident[:])

        nc.scalar.dma_start(out=norm_rows[0:PASSES, :], in_=ln1_g.rearrange("(g c) -> g c", g=PASSES))
        nc.scalar.dma_start(out=norm_rows[PASSES : 2 * PASSES, :], in_=ln1_b.rearrange("(g c) -> g c", g=PASSES))
        nc.scalar.dma_start(out=bias_row[0:1, :], in_=s_qkv_b.unsqueeze(0))
        ident_bf = const.tile([P, 2 * PASSES], BF16)
        nc.gpsimd.tensor_copy(out=ident_bf[:], in_=ident[:, 0 : 2 * PASSES])

        x_sb = []
        for s in range(SEQ):
            x_tile = const.tile([P, D], BF16, name="x%d" % s)
            x_sb.append(x_tile)

        def position(s):
            return (s + 1) % SEQ

        def load_x(s):
            if position(s) == 0:
                rows = x_res[:, 0:1, :].to_broadcast([SAMPLES, FRAMES, D])
            else:
                first = 1 + (position(s) - 1) * FRAMES
                rows = x_res[:, first : first + FRAMES, :]
            nc.sync.dma_start(out=x_sb[s][:], in_=rows)

        for s in range(EARLY_X):
            load_x(s)
        for q in range(QUADRANTS):
            nc.sync.dma_start(
                out=w_planes[QUADRANT * q : QUADRANT * q + SCALE_ROWS * PASSES, :].bitcast(I32),
                in_=s_qkv_w_scales[:, SCALE_ROWS * q : SCALE_ROWS * (q + 1), :].bitcast(I32),
            )
        w_codes = const.tile([P, PASSES, D3], U32, align_bytes=64)

        def load_w(first, last):
            cols = slice(first * BANK, last * BANK)
            for g in range(PASSES):
                words = s_qkv_w_words[g].rearrange("p n t -> p (n t)").bitcast(I32)
                nc.sync.dma_start(out=w_codes[:, g, cols].bitcast(I32), in_=words[:, cols])

        load_w(0, 3)
        load_x(3)
        load_w(3, 4)
        load_x(4)
        load_w(4, 6)
        for s in range(5, SEQ):
            load_x(s)

        bias_all = const.tile([P, D3], BF16)

        spreads = {}

        def spread_bias(i):
            spreads[i] = psum_a.tile([P, BIAS_AT_ONCE, BANK], BF16, tag="acc", name="spread%d" % i)
            for h in range(BIAS_AT_ONCE):
                first = (BIAS_AT_ONCE * i + h) * BANK
                nc.tensor.matmul(
                    out=spreads[i][:, h, :], lhsT=ones[:], rhs=bias_row[:, first : first + BANK], start=True, stop=True
                )

        def copy_bias(i):
            first = BIAS_AT_ONCE * i * BANK
            nc.scalar.copy(out=bias_all[:, first : first + BIAS_AT_ONCE * BANK], in_=spreads[i][:].rearrange("p h c -> p (h c)"))

        norm_cols = const.tile([P, PACK, 2 * PASSES], F32)

        def turn_norm_rows():
            turned = psum_a.tile([P, PACK, 2 * PASSES], F32, tag="acc")
            for t in range(PACK):
                nc.tensor.matmul(
                    out=turned[:, t, :], lhsT=norm_rows[:, t:K_PASS:PACK], rhs=ident_bf[:], start=True, stop=True
                )
            return turned

        def copy_norm_cols(turned):
            nc.scalar.copy(out=norm_cols[:], in_=turned[:])

        parts, mean_var, negmean, sumsq, var_eps, rstd, xhat, planar, grouped = {}, {}, {}, {}, {}, {}, {}, {}, {}
        y_codes, y_planes = {}, {}

        def half_sums(s, h):
            if h == 0:
                parts[s] = small.tile([P, PASSES, BN_VALUES], F32, tag="parts", name="parts%d" % s)
            nc.vector.bn_stats(out=parts[s][:, h, :], in_=x_sb[s][:, h * K_PASS : (h + 1) * K_PASS])

        def mean_and_variance(s):
            mean_var[s] = small.tile([P, 2], F32, tag="mean_var", name="mean_var%d" % s)
            nc.vector.bn_aggr(out=mean_var[s][:], in_=parts[s][:].rearrange("p h c -> p (h c)"))

        def add_eps(s):
            var_eps[s] = small.tile([P, 1], F32, tag="var_eps", name="var_eps%d" % s)
            nc.vector.tensor_scalar_add(out=var_eps[s][:], in0=mean_var[s][:, 1:2], scalar1=EPS)
            if s >= HEAD_TILES:
                negmean[s] = small.tile([P, 1], F32, tag="negmean", name="negmean%d" % s)
                nc.vector.tensor_scalar_mul(out=negmean[s][:], in0=mean_var[s][:, 0:1], scalar1=-1.0)

        def scalar_mean(s):
            negmean[s] = small.tile([P, 1], F32, tag="negmean", name="negmean%d" % s)
            unread = work.tile([P, D], BF16, tag="unread", bufs=4)
            nc.scalar.activation(
                out=unread[:], in_=x_sb[s][:], func=ACT.Identity, scale=-1.0 / D, accum_out=negmean[s][:]
            )

        def scalar_square(s):
            sumsq[s] = small.tile([P, 1], F32, tag="sumsq", name="sumsq%d" % s)
            unread = work.tile([P, D], BF16, tag="unread", bufs=4)
            nc.scalar.activation(
                out=unread[:], in_=x_sb[s][:], func=ACT.Square, bias=negmean[s][:], accum_out=sumsq[s][:]
            )

        def scalar_variance(s):
            var_eps[s] = small.tile([P, 1], F32, tag="var_eps", name="var_eps%d" % s)
            nc.scalar.activation(
                out=var_eps[s][:], in_=sumsq[s][:], func=ACT.Identity, bias=eps_col[:], scale=1.0 / D
            )

        def scalar_statistics(s):
            if s < SEQ:
                scalar_square(s)
            if s + 1 < SEQ:
                scalar_mean(s + 1)
            if s < SEQ:
                scalar_variance(s)

        def reciprocal_std(s):
            rstd[s] = small.tile([P, 1], F32, tag="rstd", name="rstd%d" % s)
            nc.gpsimd.tensor_tensor(out=rstd[s][:], in0=var_eps[s][:], in1=minus_half[:], op=ALU.pow)

        def normalise(s):
            xhat[s] = work.tile([P, PASSES, PACK, P], F32, tag="slot%d" % (s % SLOTS), name="xhat%d" % s, bufs=1, align_bytes=64)
            engine = nc.vector if s < HEAD_TILES else nc.gpsimd
            minus = s not in negmean
            engine.tensor_scalar(
                out=xhat[s][:],
                in0=x_sb[s][:].rearrange("r (g p t) -> r g t p", g=PASSES, t=PACK),
                scalar1=mean_var[s][:, 0:1] if minus else negmean[s][:],
                scalar2=rstd[s][:],
                op0=ALU.subtract if minus else ALU.add,
                op1=ALU.mult,
            )

        def transpose(s):
            planar[s] = work.tile([P, PASSES, PACK, P], BF16, tag="planar", name="planar%d" % s)
            for g in range(PASSES):
                bank = psum_t.tile([P, PACK, P], F32, tag="xt")
                for t in range(PACK):
                    nc.tensor.transpose(out=bank[:, t, :], in_=xhat[s][:, g, t, :], identity=ident[:])
                for t in range(PACK):
                    nc.scalar.activation(
                        out=planar[s][:, g, t, :],
                        in_=bank[:, t, :],
                        func=ACT.Identity,
                        scale=norm_cols[:, t, g : g + 1],
                        bias=norm_cols[:, t, PASSES + g : PASSES + g + 1],
                    )

        def regroup(s, g0, g1):
            if g0 == 0:
                grouped[s] = work.tile(
                    [P, PASSES, P, PACK], BF16, tag="slot%d" % ((s + 2) % SLOTS), name="grouped%d" % s, bufs=1, align_bytes=64
                )
            engine = nc.vector if s < VECTOR_REGROUPS else nc.gpsimd
            engine.tensor_scalar(
                out=grouped[s][:, g0:g1],
                in0=planar[s][:, g0:g1].rearrange("p g t r -> p g r t"),
                scalar1=1.0,
                scalar2=0.0,
                op0=ALU.mult,
                op1=ALU.add,
            )

        def quantise(s, g0, g1):
            if g0 == 0:
                y_codes[s] = const.tile([P, PASSES, P], U32, name="y_codes%d" % s, align_bytes=64)
                y_planes[s] = const.tile([P, PASSES, P], U8, name="y_planes%d" % s, align_bytes=64)
            nc.vector.quantize_mx(
                out=y_codes[s][:, g0:g1].rearrange("p g r -> p (g r)").bitcast(FP8X4),
                scales=y_planes[s][:, g0:g1].rearrange("p g r -> p (g r)"),
                in_=grouped[s][:, g0:g1].rearrange("p g r t -> p (g r t)"),
            )

        accs, results_of = {}, {}

        def passes(s, first, banks=STORE_BANKS, by_pass=False):
            js = range(first, first + banks)
            for j in js:
                accs[s, j] = psum_a.tile([P, BANK], F32, tag="acc", name="acc%d_%d" % (s, j))
            order = [(j, g) for g in range(PASSES) for j in js] if by_pass else [(j, g) for j in js for g in range(PASSES)]
            for j, g in order:
                cols = slice(j * BANK, (j + 1) * BANK)
                nc.tensor.matmul_mx(
                    out=accs[s, j][:],
                    lhsT=y_codes[s][:, g, :].bitcast(FP8X4),
                    lhsT_scale=y_planes[s][:, g, :],
                    rhs=w_codes[:, g, cols].bitcast(FP8X4),
                    rhs_scale=w_planes[SCALE_ROWS * g : P, cols],
                    start=(g == 0),
                    stop=(g == PASSES - 1),
                )

        def empty(s, j):
            cols = slice(j * BANK, (j + 1) * BANK)
            half, slot = divmod(j, STORE_BANKS)
            if slot == 0:
                result = results.tile([P, STORE_BANKS, BANK], F32, tag="result", name="result%d_%d" % (s, half))
                results_of[s, half] = result
            result = results_of[s, half]
            nc.vector.tensor_tensor(out=result[:, slot, :], in0=accs[s, j][:], in1=bias_all[:, cols], op=ALU.add)
            if s >= SEQ - 3:
                nc.sync.dma_start(out=out[:, position(s), cols], in_=result[:, slot, :])
            elif slot == STORE_BANKS - 1:
                nc.sync.dma_start(
                    out=out[:, position(s), half * STORE_BANKS * BANK : (half + 1) * STORE_BANKS * BANK],
                    in_=result[:].rearrange("p j c -> p (j c)"),
                )

        def multiply(s, first):
            passes(s, first)
            for j in range(first, first + STORE_BANKS):
                empty(s, j)

        turned = turn_norm_rows()
        spread_bias(0)
        spread_bias(1)
        half_sums(0, 0)
        half_sums(0, 1)
        scalar_mean(1)
        copy_norm_cols(turned)
        mean_and_variance(0)
        add_eps(0)
        reciprocal_std(0)
        half_sums(2, 0)
        normalise(0)
        scalar_square(1)
        scalar_variance(1)
        reciprocal_std(1)
        transpose(0)
        copy_bias(0)
        spread_bias(2)
        half_sums(2, 1)
        mean_and_variance(2)
        add_eps(2)
        reciprocal_std(2)
        normalise(1)
        regroup(0, 0, 1)
        transpose(1)
        regroup(0, 1, 2)
        quantise(0, 0, 1)
        quantise(0, 1, 2)
        copy_bias(2)
        copy_bias(1)
        normalise(2)
        passes(0, 0, by_pass=True)
        regroup(1, 0, 1)
        regroup(1, 1, 2)
        quantise(1, 0, 1)
        empty(0, 0)
        quantise(1, 1, 2)
        half_sums(3, 0)
        empty(0, 1)
        half_sums(3, 1)
        empty(0, 2)
        mean_and_variance(3)
        transpose(2)
        passes(1, 0, by_pass=True)
        empty(1, 0)
        add_eps(3)
        empty(1, 1)
        empty(1, 2)
        scalar_mean(4)
        scalar_square(4)
        scalar_variance(4)
        scalar_mean(5)
        regroup(2, 0, PASSES)
        reciprocal_std(3)
        normalise(3)
        for j in range(STORE_BANKS, BANKS):
            for tile in range(2):
                passes(tile, j, 1)
                empty(tile, j)
            if j == STORE_BANKS:
                quantise(2, 0, PASSES)
        transpose(3)
        scalar_statistics(5)
        reciprocal_std(4)
        normalise(4)
        regroup(3, 0, PASSES)

        for s in range(2, SEQ):
            multiply(s, 0)
            if s + AHEAD_QUANTISE < SEQ:
                quantise(s + AHEAD_QUANTISE, 0, PASSES)
            if s < 3:
                multiply(s, STORE_BANKS)
            if s + AHEAD_TRANSPOSE < SEQ:
                transpose(s + AHEAD_TRANSPOSE)
            scalar_statistics(s + AHEAD_STATISTICS)
            if s + AHEAD_NORMALISE < SEQ:
                reciprocal_std(s + AHEAD_NORMALISE)
                normalise(s + AHEAD_NORMALISE)
            if s + AHEAD_TRANSPOSE < SEQ:
                regroup(s + AHEAD_TRANSPOSE, 0, PASSES)
            if s >= 3:
                multiply(s, STORE_BANKS)
